import numpy as np
import ml_dtypes


def mxq(x, axis, fmt="e4m3"):
    dtype, down = {"e4m3": (ml_dtypes.float8_e4m3fn, 7), "e5m2": (ml_dtypes.float8_e5m2, 14)}[fmt]
    v = np.moveaxis(np.asarray(x, np.float32).astype(ml_dtypes.bfloat16).astype(np.float64), axis, -1)
    blocks = v.reshape(v.shape[:-1] + (-1, 32))
    amax = np.abs(blocks).max(-1, keepdims=True)
    byte = np.maximum(np.where(amax > 0, np.frexp(amax)[1] - 1 + 127, 0) - down, 1)
    scale = np.exp2(byte - 127.0)
    codes = (blocks / scale).astype(np.float32).astype(dtype).astype(np.float64)
    return np.moveaxis((codes * scale).reshape(v.shape), -1, axis)


WIDE = False


def mx_kscale(k):
    if not WIDE:
        return np.ones(k)
    levels = np.array([10, -10, 5, -5, 0])
    if k % 512:
        return np.exp2(np.random.permutation(np.resize(levels, k // 32))).repeat(32)
    a = np.empty((k // 512, 16))
    for p in range(k // 512):
        a[p, :8] = np.random.permutation(np.resize(levels, 8))
        for g in range(8):
            far = levels[np.abs(levels - a[p, g]) >= 10]
            a[p, g + 8] = far[np.random.randint(len(far))]
    return np.exp2(a.ravel()).repeat(32)


BF16 = ml_dtypes.bfloat16


def bf(x):
    return np.asarray(x, np.float32).astype(BF16)


def f64(x):
    return np.asarray(x).astype(np.float64)


B, NI, NK, NJ, C_Z, C_H = 1, 512, 512, 512, 128, 8
EPS = 1e-5
KEEP = 0.85


def layer_norm(x, w, b):
    mu = x.mean(-1, keepdims=True)
    var = ((x - mu) ** 2).mean(-1, keepdims=True)
    return (x - mu) / np.sqrt(var + EPS) * w + b


def setup_inputs():
    s = mx_kscale(NK)
    return {"a_gated": bf(np.random.standard_normal((B, NI, NK, C_H)) * 0.55 * s[None, None, :, None]),
            "b_gated": bf(np.random.standard_normal((B, NK, NJ, C_H)) * 0.55 / s[None, :, None, None]),
            "mask_ik": bf(np.random.random((B, NI, NK)) < KEEP),
            "mask_kj": bf(np.random.random((B, NK, NJ)) < KEEP),
            "ln_out_w": bf(1.0 + 0.1 * np.random.standard_normal(C_H)),
            "ln_out_b": bf(0.1 * np.random.standard_normal(C_H))}


def reference(a_gated, b_gated, mask_ik, mask_kj, ln_out_w, ln_out_b):
    a = f64(mask_ik)[..., None] * f64(a_gated)
    b = f64(mask_kj)[..., None] * f64(b_gated)
    at = a.transpose(0, 3, 1, 2)
    bt = b.transpose(0, 3, 1, 2)
    x = (mxq(at, 3, "e4m3") @ mxq(bt, 2, "e4m3")).transpose(0, 2, 3, 1)
    return layer_norm(x, f64(ln_out_w), f64(ln_out_b))

@@ -1,0 +1,354 @@
+from contextlib import ExitStack
+
+import concourse.mybir as mybir
+from concourse.masks import make_identity
+
+FP8X4 = mybir.dt.float8_e4m3fn_x4
+BF16 = mybir.dt.bfloat16
+F32 = mybir.dt.float32
+U32 = mybir.dt.uint32
+U8 = mybir.dt.uint8
+ALU = mybir.AluOpType
+ACT = mybir.ActivationFunctionType
+
+P = 128
+PACK = 4
+NI = 512
+NK = P * PACK
+NJ = 512
+ND = 8
+HALF = ND // 2
+I_TILES = NI // P
+JC = 128
+J_CHUNKS = NJ // JC
+PAIR = 2
+I_PAIRS = I_TILES // PAIR
+BLOCK = PAIR * JC
+LOADS_AHEAD = 3
+EPS = 1e-5
+
+FLOPS = 2 * NI * NJ * NK * ND
+
+
+def tile_trianglemultiplicativeupdate_pa_kernel(
+    tc, a_gated, b_gated, mask_ik, mask_kj, ln_out_w, ln_out_b, out
+):
+    nc = tc.nc
+
+    a_rows = a_gated.rearrange("b (n p) k d -> (b n) p (k d)", p=P)
+    mik_rows = mask_ik.rearrange("b (n p) k -> p (b n) k", p=P)
+    b_rows = b_gated.rearrange("b (p t) j d -> p (b t) (j d)", t=PACK)
+    mkj_rows = mask_kj.rearrange("b (p t) j -> p (b t) j", t=PACK)
+    out_rows = out.rearrange("b (n p) j d -> (b n) p (j d)", p=P)
+
+    with ExitStack() as ctx:
+        ctx.enter_context(tc.manual_schedule())
+        consts = ctx.enter_context(tc.tile_pool(name="consts", bufs=1))
+        keep = ctx.enter_context(tc.tile_pool(name="keep", bufs=1))
+        a_in = ctx.enter_context(tc.tile_pool(name="a_in", bufs=LOADS_AHEAD))
+        a_work = ctx.enter_context(tc.tile_pool(name="a_work", bufs=2))
+        b_in = ctx.enter_context(tc.tile_pool(name="b_in", bufs=LOADS_AHEAD))
+        b_work = ctx.enter_context(tc.tile_pool(name="b_work", bufs=3))
+        b_mx = ctx.enter_context(tc.tile_pool(name="b_mx", bufs=J_CHUNKS))
+        ln = ctx.enter_context(tc.tile_pool(name="ln", bufs=4))
+        planes = ctx.enter_context(tc.tile_pool(name="planes", bufs=2))
+        results = ctx.enter_context(tc.tile_pool(name="results", bufs=4))
+        psum = ctx.enter_context(tc.psum_pool(name="psum", bufs=8))
+
+        ident_f32 = consts.tile([P, P], F32)
+        make_identity(nc, ident_f32[:])
+        ident_bf16 = consts.tile([P, P], BF16)
+        make_identity(nc, ident_bf16[:])
+        w_bf16 = consts.tile([P, ND], BF16)
+        nc.gpsimd.dma_start(out=w_bf16[:], in_=ln_out_w.partition_broadcast(P))
+        bias_bf16 = consts.tile([P, ND], BF16)
+        nc.gpsimd.dma_start(out=bias_bf16[:], in_=ln_out_b.partition_broadcast(P))
+        eps_col = consts.tile([P, 1], F32)
+        nc.vector.memset(eps_col[:], EPS)
+        w_col = consts.tile([P, ND], F32)
+        bias_col = consts.tile([P, ND], F32)
+
+        a_codes = keep.tile([P, I_TILES, ND * P], U32, align_bytes=64)
+        a_scales = keep.tile([P, I_TILES, ND * P], U8, align_bytes=64)
+        mik = keep.tile([P, I_TILES, NK], BF16)
+        mikT = keep.tile([P, I_TILES, P, PACK], BF16)
+        mkj = keep.tile([P, PACK, NJ], BF16)
+        mkj_grouped = keep.tile([P, NJ, PACK], BF16)
+        a_raw_tiles = []
+        a_grouped_tiles = []
+        b_raw_tiles = []
+        b_grouped_tiles = []
+        quantised_b = []
+
+        def load_a(it):
+            nc.sync.dma_start(out=mik[:, it, :], in_=mik_rows[:, it, :])
+            a_raw = a_in.tile([P, NK * ND], BF16)
+            nc.sync.dma_start(out=a_raw[:], in_=a_rows[it])
+            a_raw_tiles.append(a_raw)
+
+        def load_b(jc):
+            b_raw = b_in.tile([P, PACK, JC * ND], BF16)
+            nc.sync.dma_start(out=b_raw[:], in_=b_rows[:, :, jc * JC * ND : (jc + 1) * JC * ND])
+            b_raw_tiles.append(b_raw)
+
+        def transpose_a(it):
+            a_raw = a_raw_tiles[it]
+            maskT_ps = psum.tile([P, PACK, P], BF16, tag="bank")
+            for t in range(PACK):
+                nc.tensor.transpose(maskT_ps[:, t, :], mik[:, it, t:NK:PACK], ident_bf16[:])
+            nc.scalar.copy(out=mikT[:, it, :, :], in_=maskT_ps[:].rearrange("p t i -> p i t"))
+
+            a_words = a_raw[:].bitcast(F32).rearrange("p (k w) -> p k w", w=HALF)
+            a_grouped = a_work.tile([P, ND, P, PACK], BF16, align_bytes=64)
+            a_grouped_tiles.append(a_grouped)
+            pair_mask = mikT[:, it, :, :].unsqueeze(1).to_broadcast([P, 2, P, PACK])
+            for w in range(HALF):
+                aT_ps = psum.tile([P, PACK * P], F32, tag="bank")
+                for t in range(PACK):
+                    nc.tensor.transpose(
+                        aT_ps[:, t * P : (t + 1) * P], a_words[:, t:NK:PACK, w], ident_f32[:]
+                    )
+                pair = a_grouped[:, 2 * w : 2 * w + 2, :, :]
+                pair_T = aT_ps[:].bitcast(BF16).rearrange("p (t i e) -> p e i t", t=PACK, e=2)
+                if w == 0:
+                    nc.scalar.copy(out=pair, in_=pair_T)
+                else:
+                    nc.vector.tensor_tensor(out=pair, in0=pair_T, in1=pair_mask, op=ALU.mult)
+
+        def mask_first_pair_of_a(it):
+            pair = a_grouped_tiles[it][:, 0:2, :, :]
+            pair_mask = mikT[:, it, :, :].unsqueeze(1).to_broadcast([P, 2, P, PACK])
+            nc.vector.tensor_tensor(out=pair, in0=pair, in1=pair_mask, op=ALU.mult)
+
+        def quantise_a(it):
+            nc.vector.quantize_mx(
+                out=a_codes[:, it, :].bitcast(FP8X4),
+                scales=a_scales[:, it, :],
+                in_=a_grouped_tiles[it][:].rearrange("p d i t -> p (d i t)"),
+            )
+
+        def prepare_a_pair(ip):
+            tiles = range(ip * PAIR, (ip + 1) * PAIR)
+            for it in tiles:
+                transpose_a(it)
+                if it + LOADS_AHEAD < I_TILES:
+                    load_a(it + LOADS_AHEAD)
+            for it in tiles:
+                mask_first_pair_of_a(it)
+            for it in tiles:
+                quantise_a(it)
+
+        def regroup_b(jc):
+            b_raw = b_raw_tiles[jc]
+            b_grouped = b_work.tile([P, ND, JC, PACK], BF16, align_bytes=64)
+            src = b_raw[:].rearrange("p t (j d) -> p j t d", d=ND)
+            dst = b_grouped[:].rearrange("p d j t -> p j t d")
+            for h in range(2):
+                half = slice(h * HALF, (h + 1) * HALF)
+                nc.scalar.copy(out=dst[:, :, :, half], in_=src[:, :, :, half])
+            b_grouped_tiles.append(b_grouped)
+            if jc + LOADS_AHEAD < J_CHUNKS:
+                load_b(jc + LOADS_AHEAD)
+
+        def quantise_b(jc):
+            b_grouped = b_grouped_tiles[jc]
+            b_flat = b_grouped[:].rearrange("p d j t -> p d (j t)")
+            nc.vector.tensor_tensor(
+                out=b_flat,
+                in0=b_flat,
+                in1=mkj_grouped[:, jc * JC : (jc + 1) * JC, :]
+                .rearrange("p j t -> p (j t)")
+                .unsqueeze(1)
+                .to_broadcast([P, ND, JC * PACK]),
+                op=ALU.mult,
+            )
+            b_codes = b_mx.tile([P, ND, JC], U32, align_bytes=64)
+            b_scales = b_mx.tile([P, ND, JC], U8, align_bytes=64)
+            nc.vector.quantize_mx(
+                out=b_codes[:].rearrange("p d j -> p (d j)").bitcast(FP8X4),
+                scales=b_scales[:].rearrange("p d j -> p (d j)"),
+                in_=b_grouped[:].rearrange("p d j t -> p (d j t)"),
+            )
+            quantised_b.append((b_codes, b_scales))
+
+        blocks = [(ip, jc) for jc in range(J_CHUNKS) for ip in range(I_PAIRS)]
+        tiles_of = [dict() for block in blocks]
+
+        def product(where, block, n, d, first, last):
+            ip, jc = block
+            it = ip * PAIR + n
+            b_codes, b_scales = quantised_b[jc]
+            nc.tensor.matmul_mx(
+                out=where[:, n * JC : (n + 1) * JC],
+                lhsT=a_codes[:, it, d * P : (d + 1) * P].bitcast(FP8X4),
+                lhsT_scale=a_scales[:, it, d * P : (d + 1) * P],
+                rhs=b_codes[:, d, :].bitcast(FP8X4),
+                rhs_scale=b_scales[:, d, :],
+                start=first,
+                stop=last,
+            )
+
+        def products_of_two_channels(block, q):
+            x_ps = psum.tile([P, 2, BLOCK], F32, tag="bank")
+            for e in range(2):
+                for n in range(PAIR):
+                    product(x_ps[:, e, :], block, n, 2 * q + e, True, True)
+            return x_ps
+
+        def sums_and_squares(m):
+            sum_ps = psum.tile([P, BLOCK], F32, tag="bank")
+            for n in range(PAIR):
+                for d in range(ND):
+                    product(sum_ps, blocks[m], n, d, d == 0, d == ND - 1)
+            mean_sq = ln.tile([P, BLOCK], F32)
+            nc.scalar.activation(out=mean_sq[:], in_=sum_ps[:], func=ACT.Square, scale=1.0 / ND)
+            neg_mean = ln.tile([P, BLOCK], F32)
+            nc.scalar.activation(out=neg_mean[:], in_=sum_ps[:], func=ACT.Copy, scale=-1.0 / ND)
+            squares = planes.tile([P, ND, BLOCK], F32)
+            for q in range(HALF):
+                x_ps = products_of_two_channels(blocks[m], q)
+                nc.scalar.activation(out=squares[:, 2 * q : 2 * q + 2, :], in_=x_ps[:], func=ACT.Square)
+            tiles_of[m].update(mean_sq=mean_sq, neg_mean=neg_mean, squares=squares)
+
+        def add_squares(m):
+            squares = tiles_of[m]["squares"]
+            sum_sq_T_ps = psum.tile([P, BLOCK], F32, tag="bank")
+            for n in range(PAIR):
+                cols = slice(n * JC, (n + 1) * JC)
+                for d in range(ND):
+                    nc.tensor.matmul(
+                        out=sum_sq_T_ps[:, cols],
+                        lhsT=squares[:, d, cols],
+                        rhs=ident_f32[:],
+                        is_transpose=True,
+                        start=(d == 0),
+                        stop=(d == ND - 1),
+                    )
+            tiles_of[m].update(sum_sq_T_ps=sum_sq_T_ps)
+
+        def copy_sum_of_squares(m):
+            sum_sq_T = ln.tile([P, BLOCK], F32)
+            nc.scalar.copy(out=sum_sq_T[:], in_=tiles_of[m]["sum_sq_T_ps"][:])
+            tiles_of[m].update(sum_sq_T=sum_sq_T)
+
+        def transpose_sum_of_squares_back(m):
+            sum_sq_T = tiles_of[m]["sum_sq_T"]
+            sum_sq_ps = psum.tile([P, BLOCK], F32, tag="bank")
+            for n in range(PAIR):
+                cols = slice(n * JC, (n + 1) * JC)
+                nc.tensor.transpose(sum_sq_ps[:, cols], sum_sq_T[:, cols], ident_f32[:])
+            tiles_of[m].update(sum_sq_ps=sum_sq_ps)
+
+        def variance(m):
+            var = ln.tile([P, BLOCK], F32)
+            nc.vector.scalar_tensor_tensor(
+                out=var[:],
+                in0=tiles_of[m]["sum_sq_ps"][:],
+                scalar=1.0 / ND,
+                in1=tiles_of[m]["mean_sq"][:],
+                op0=ALU.mult,
+                op1=ALU.subtract,
+            )
+            tiles_of[m].update(var=var)
+
+        def reciprocal_std(m):
+            rstd = ln.tile([P, BLOCK], F32)
+            nc.scalar.activation(
+                out=rstd[:], in_=tiles_of[m]["var"][:], func=ACT.Abs_reciprocal_sqrt, bias=eps_col[:, 0:1]
+            )
+            tiles_of[m].update(rstd=rstd)
+
+        def minus_mean_times_rstd(m):
+            neg_mean_rstd = ln.tile([P, BLOCK], F32)
+            nc.vector.tensor_tensor(
+                out=neg_mean_rstd[:], in0=tiles_of[m]["neg_mean"][:], in1=tiles_of[m]["rstd"][:], op=ALU.mult
+            )
+            tiles_of[m].update(neg_mean_rstd=neg_mean_rstd)
+
+        def shifts(m):
+            shift = planes.tile([P, ND, BLOCK], F32)
+            for d in range(HALF):
+                nc.scalar.activation(
+                    out=shift[:, d, :],
+                    in_=tiles_of[m]["neg_mean_rstd"][:],
+                    func=ACT.Identity,
+                    scale=w_col[:, d : d + 1],
+                    bias=bias_col[:, d : d + 1],
+                )
+            for d in range(HALF, ND):
+                nc.vector.tensor_scalar(
+                    out=shift[:, d, :],
+                    in0=tiles_of[m]["neg_mean_rstd"][:],
+                    scalar1=w_col[:, d : d + 1],
+                    scalar2=bias_col[:, d : d + 1],
+                    op0=ALU.mult,
+                    op1=ALU.add,
+                )
+            tiles_of[m].update(shift=shift)
+
+        def scale_products(m):
+            scaled = planes.tile([P, ND, BLOCK], F32, bufs=1)
+            for q in range(HALF):
+                x_ps = products_of_two_channels(blocks[m], q)
+                for e in range(2):
+                    d = 2 * q + e
+                    nc.vector.scalar_tensor_tensor(
+                        out=scaled[:, d, :],
+                        in0=x_ps[:, e, :],
+                        scalar=w_col[:, d : d + 1],
+                        in1=tiles_of[m]["rstd"][:],
+                        op0=ALU.mult,
+                        op1=ALU.mult,
+                    )
+            tiles_of[m].update(scaled=scaled)
+
+        def add_shifts_and_store(m):
+            ip, jc = blocks[m]
+            for n in range(PAIR):
+                cols = slice(n * JC, (n + 1) * JC)
+                result = results.tile([P, JC, ND], F32)
+                nc.vector.tensor_tensor(
+                    out=result[:].rearrange("p (c e) d -> p c d e", e=2),
+                    in0=tiles_of[m]["scaled"][:, :, cols].rearrange("p d (c e) -> p c d e", e=2),
+                    in1=tiles_of[m]["shift"][:, :, cols].rearrange("p d (c e) -> p c d e", e=2),
+                    op=ALU.add,
+                )
+                nc.sync.dma_start(
+                    out=out_rows[ip * PAIR + n, :, jc * JC * ND : (jc + 1) * JC * ND],
+                    in_=result[:].rearrange("p j d -> p (j d)"),
+                )
+
+        load_a(0)
+        load_a(1)
+        nc.sync.dma_start(out=mkj[:], in_=mkj_rows)
+        load_b(0)
+        load_a(2)
+        load_b(1)
+        load_b(2)
+
+        prepare_a_pair(0)
+        nc.scalar.copy(out=mkj_grouped[:], in_=mkj[:].rearrange("p t j -> p j t"))
+        regroup_b(0)
+        quantise_b(0)
+        prepare_a_pair(1)
+        for jc in range(1, J_CHUNKS):
+            regroup_b(jc)
+            quantise_b(jc)
+        nc.vector.tensor_copy(out=w_col[:], in_=w_bf16[:])
+        nc.vector.tensor_copy(out=bias_col[:], in_=bias_bf16[:])
+
+        def stage(work, m):
+            if 0 <= m < len(blocks):
+                work(m)
+
+        for m in range(-4, len(blocks)):
+            stage(scale_products, m)
+            stage(add_squares, m + 2)
+            stage(copy_sum_of_squares, m + 2)
+            stage(minus_mean_times_rstd, m + 1)
+            stage(add_shifts_and_store, m)
+            stage(sums_and_squares, m + 4)
+            stage(transpose_sum_of_squares_back, m + 2)
+            stage(variance, m + 2)
+            stage(reciprocal_std, m + 2)
+            stage(shifts, m + 1)

@@ -24,8 +24,13 @@ J_CHUNKS = NJ // JC
 PAIR = 2
 I_PAIRS = I_TILES // PAIR
 BLOCK = PAIR * JC
-LOADS_AHEAD = 3
+SLABS = 16
 EPS = 1e-5
+A_ON_SCALAR = ((0, 2), (0, 2), (0, 1, 2, 3), ())
+B_ON_VECTOR = (0, 2)
+B_ON_GPSIMD = ()
+SHIFTS_ON_SCALAR = 6
+B_PARTS = 2
 
 FLOPS = 2 * NI * NJ * NK * ND
 
@@ -45,16 +50,41 @@ def tile_trianglemultiplicativeupdate_pa_kernel(
         ctx.enter_context(tc.manual_schedule())
         consts = ctx.enter_context(tc.tile_pool(name="consts", bufs=1))
         keep = ctx.enter_context(tc.tile_pool(name="keep", bufs=1))
-        a_in = ctx.enter_context(tc.tile_pool(name="a_in", bufs=LOADS_AHEAD))
-        a_work = ctx.enter_context(tc.tile_pool(name="a_work", bufs=2))
-        b_in = ctx.enter_context(tc.tile_pool(name="b_in", bufs=LOADS_AHEAD))
-        b_work = ctx.enter_context(tc.tile_pool(name="b_work", bufs=3))
+        slabs = ctx.enter_context(tc.tile_pool(name="slabs", bufs=SLABS))
         b_mx = ctx.enter_context(tc.tile_pool(name="b_mx", bufs=J_CHUNKS))
-        ln = ctx.enter_context(tc.tile_pool(name="ln", bufs=4))
-        planes = ctx.enter_context(tc.tile_pool(name="planes", bufs=2))
+        ln = ctx.enter_context(tc.tile_pool(name="ln", bufs=3))
         results = ctx.enter_context(tc.tile_pool(name="results", bufs=4))
-        psum = ctx.enter_context(tc.psum_pool(name="psum", bufs=8))
+        psum = ctx.enter_context(tc.psum_pool(name="psum", bufs=6))
+        stats = ctx.enter_context(tc.psum_pool(name="stats", bufs=2))
 
+        mik = keep.tile([P, I_TILES, NK], BF16)
+        mkj = keep.tile([P, PACK, NJ], BF16)
+        a_raw_tiles = []
+        b_raw_tiles = []
+
+        def load_a(it):
+            nc.sync.dma_start(out=mik[:, it, :], in_=mik_rows[:, it, :])
+            a_raw = slabs.tile([P, NK * ND], BF16, tag="slab", align_bytes=64)
+            nc.sync.dma_start(out=a_raw[:], in_=a_rows[it])
+            a_raw_tiles.append(a_raw)
+
+        def load_b(jc):
+            b_raw = slabs.tile([P, PACK, JC * ND], BF16, tag="slab", align_bytes=64)
+            nc.sync.dma_start(out=b_raw[:], in_=b_rows[:, :, jc * JC * ND : (jc + 1) * JC * ND])
+            b_raw_tiles.append(b_raw)
+
+        load_a(0)
+        nc.sync.dma_start(out=mkj[:], in_=mkj_rows)
+        load_b(0)
+        load_a(1)
+        load_a(2)
+        load_b(1)
+        load_a(3)
+        load_b(2)
+        load_b(3)
+
+        eps_col = consts.tile([P, 1], F32)
+        nc.vector.memset(eps_col[:], EPS)
         ident_f32 = consts.tile([P, P], F32)
         make_identity(nc, ident_f32[:])
         ident_bf16 = consts.tile([P, P], BF16)
@@ -63,111 +93,108 @@ def tile_trianglemultiplicativeupdate_pa_kernel(
         nc.gpsimd.dma_start(out=w_bf16[:], in_=ln_out_w.partition_broadcast(P))
         bias_bf16 = consts.tile([P, ND], BF16)
         nc.gpsimd.dma_start(out=bias_bf16[:], in_=ln_out_b.partition_broadcast(P))
-        eps_col = consts.tile([P, 1], F32)
-        nc.vector.memset(eps_col[:], EPS)
         w_col = consts.tile([P, ND], F32)
         bias_col = consts.tile([P, ND], F32)
+        table_col = consts.tile([P, 1], F32)
+        nc.scalar.activation(out=table_col[:], in_=eps_col[:], func=ACT.Abs_reciprocal_sqrt)
 
-        a_codes = keep.tile([P, I_TILES, ND * P], U32, align_bytes=64)
-        a_scales = keep.tile([P, I_TILES, ND * P], U8, align_bytes=64)
-        mik = keep.tile([P, I_TILES, NK], BF16)
+        a_codes = keep.tile([P, I_PAIRS, ND, PAIR * P], U32, align_bytes=64)
+        a_scales = keep.tile([P, I_PAIRS, ND, PAIR * P], U8, align_bytes=64)
         mikT = keep.tile([P, I_TILES, P, PACK], BF16)
-        mkj = keep.tile([P, PACK, NJ], BF16)
         mkj_grouped = keep.tile([P, NJ, PACK], BF16)
-        a_raw_tiles = []
-        a_grouped_tiles = []
-        b_raw_tiles = []
-        b_grouped_tiles = []
+        a_grouped_pairs = [[] for ip in range(I_PAIRS)]
+        b_grouped_tiles = {}
         quantised_b = []
 
-        def load_a(it):
-            nc.sync.dma_start(out=mik[:, it, :], in_=mik_rows[:, it, :])
-            a_raw = a_in.tile([P, NK * ND], BF16)
-            nc.sync.dma_start(out=a_raw[:], in_=a_rows[it])
-            a_raw_tiles.append(a_raw)
+        def pair_of_a(ip, w):
+            e = 2 * (w % 2)
+            return a_grouped_pairs[ip][w // 2][:, e : e + 2, :, :]
 
-        def load_b(jc):
-            b_raw = b_in.tile([P, PACK, JC * ND], BF16)
-            nc.sync.dma_start(out=b_raw[:], in_=b_rows[:, :, jc * JC * ND : (jc + 1) * JC * ND])
-            b_raw_tiles.append(b_raw)
-
-        def transpose_a(it):
-            a_raw = a_raw_tiles[it]
+        def turn_mask(ip, n):
+            it = ip * PAIR + n
             maskT_ps = psum.tile([P, PACK, P], BF16, tag="bank")
             for t in range(PACK):
                 nc.tensor.transpose(maskT_ps[:, t, :], mik[:, it, t:NK:PACK], ident_bf16[:])
             nc.scalar.copy(out=mikT[:, it, :, :], in_=maskT_ps[:].rearrange("p t i -> p i t"))
 
-            a_words = a_raw[:].bitcast(F32).rearrange("p (k w) -> p k w", w=HALF)
-            a_grouped = a_work.tile([P, ND, P, PACK], BF16, align_bytes=64)
-            a_grouped_tiles.append(a_grouped)
+        def turn_a(ip, n, ws=range(HALF)):
+            it = ip * PAIR + n
+            if not a_grouped_pairs[ip]:
+                for h in range(2):
+                    a_half = slabs.tile([P, HALF, PAIR * P, PACK], BF16, tag="slab", align_bytes=64)
+                    a_grouped_pairs[ip].append(a_half)
+            a_words = a_raw_tiles[it][:].bitcast(F32).rearrange("p (k w) -> p k w", w=HALF)
             pair_mask = mikT[:, it, :, :].unsqueeze(1).to_broadcast([P, 2, P, PACK])
-            for w in range(HALF):
+            for w in ws:
                 aT_ps = psum.tile([P, PACK * P], F32, tag="bank")
                 for t in range(PACK):
                     nc.tensor.transpose(
                         aT_ps[:, t * P : (t + 1) * P], a_words[:, t:NK:PACK, w], ident_f32[:]
                     )
-                pair = a_grouped[:, 2 * w : 2 * w + 2, :, :]
+                pair = pair_of_a(ip, w)[:, :, n * P : (n + 1) * P, :]
                 pair_T = aT_ps[:].bitcast(BF16).rearrange("p (t i e) -> p e i t", t=PACK, e=2)
-                if w == 0:
+                if w in A_ON_SCALAR[it]:
                     nc.scalar.copy(out=pair, in_=pair_T)
                 else:
                     nc.vector.tensor_tensor(out=pair, in0=pair_T, in1=pair_mask, op=ALU.mult)
 
-        def mask_first_pair_of_a(it):
-            pair = a_grouped_tiles[it][:, 0:2, :, :]
-            pair_mask = mikT[:, it, :, :].unsqueeze(1).to_broadcast([P, 2, P, PACK])
-            nc.vector.tensor_tensor(out=pair, in0=pair, in1=pair_mask, op=ALU.mult)
+        def mask_a(ip, h):
+            for w in range(2 * h, 2 * h + 2):
+                tiles = [n for n in range(PAIR) if w in A_ON_SCALAR[ip * PAIR + n]]
+                if not tiles:
+                    continue
+                i_cols = slice(tiles[0] * P, (tiles[-1] + 1) * P)
+                pair = pair_of_a(ip, w)[:, :, i_cols, :].rearrange("p e i t -> p e (i t)")
+                pair_mask = (
+                    mikT[:, ip * PAIR + tiles[0] : ip * PAIR + tiles[-1] + 1, :, :]
+                    .rearrange("p n i t -> p (n i t)")
+                    .unsqueeze(1)
+                    .to_broadcast([P, 2, len(tiles) * P * PACK])
+                )
+                nc.vector.tensor_tensor(out=pair, in0=pair, in1=pair_mask, op=ALU.mult)
 
-        def quantise_a(it):
+        def quantise_a(ip, h):
+            half = slice(h * HALF, (h + 1) * HALF)
             nc.vector.quantize_mx(
-                out=a_codes[:, it, :].bitcast(FP8X4),
-                scales=a_scales[:, it, :],
-                in_=a_grouped_tiles[it][:].rearrange("p d i t -> p (d i t)"),
+                out=a_codes[:, ip, half, :].rearrange("p d i -> p (d i)").bitcast(FP8X4),
+                scales=a_scales[:, ip, half, :].rearrange("p d i -> p (d i)"),
+                in_=a_grouped_pairs[ip][h][:].rearrange("p d i t -> p (d i t)"),
             )
 
-        def prepare_a_pair(ip):
-            tiles = range(ip * PAIR, (ip + 1) * PAIR)
-            for it in tiles:
-                transpose_a(it)
-                if it + LOADS_AHEAD < I_TILES:
-                    load_a(it + LOADS_AHEAD)
-            for it in tiles:
-                mask_first_pair_of_a(it)
-            for it in tiles:
-                quantise_a(it)
+        def regroup_b(jc, h):
+            if h == 0:
+                b_grouped = slabs.tile([P, ND, JC, PACK], BF16, tag="slab", align_bytes=64)
+                b_grouped_tiles[jc] = b_grouped
+            half = slice(h * HALF, (h + 1) * HALF)
+            src = b_raw_tiles[jc][:].rearrange("p t (j d) -> p j t d", d=ND)[:, :, :, half]
+            dst = b_grouped_tiles[jc][:].rearrange("p d j t -> p j t d")[:, :, :, half]
+            mask = mkj[:, :, jc * JC : (jc + 1) * JC].rearrange("p t j -> p j t")
+            mask = mask.unsqueeze(3).to_broadcast([P, JC, PACK, HALF])
+            if jc in B_ON_VECTOR:
+                nc.vector.tensor_tensor(out=dst, in0=src, in1=mask, op=ALU.mult)
+            elif jc in B_ON_GPSIMD:
+                for c in range(0, JC, JC // B_PARTS):
+                    cols = slice(c, c + JC // B_PARTS)
+                    nc.gpsimd.tensor_tensor(out=dst[:, cols], in0=src[:, cols], in1=mask[:, cols], op=ALU.mult)
+            else:
+                nc.scalar.copy(out=dst, in_=src)
 
-        def regroup_b(jc):
-            b_raw = b_raw_tiles[jc]
-            b_grouped = b_work.tile([P, ND, JC, PACK], BF16, align_bytes=64)
-            src = b_raw[:].rearrange("p t (j d) -> p j t d", d=ND)
-            dst = b_grouped[:].rearrange("p d j t -> p j t d")
-            for h in range(2):
-                half = slice(h * HALF, (h + 1) * HALF)
-                nc.scalar.copy(out=dst[:, :, :, half], in_=src[:, :, :, half])
-            b_grouped_tiles.append(b_grouped)
-            if jc + LOADS_AHEAD < J_CHUNKS:
-                load_b(jc + LOADS_AHEAD)
+        def mask_b(jc):
+            if jc in B_ON_VECTOR or jc in B_ON_GPSIMD:
+                return
+            b_flat = b_grouped_tiles[jc][:].rearrange("p d j t -> p d (j t)")
+            mask = mkj_grouped[:, jc * JC : (jc + 1) * JC, :].rearrange("p j t -> p (j t)")
+            nc.vector.tensor_tensor(
+                out=b_flat, in0=b_flat, in1=mask.unsqueeze(1).to_broadcast([P, ND, JC * PACK]), op=ALU.mult
+            )
 
         def quantise_b(jc):
-            b_grouped = b_grouped_tiles[jc]
-            b_flat = b_grouped[:].rearrange("p d j t -> p d (j t)")
-            nc.vector.tensor_tensor(
-                out=b_flat,
-                in0=b_flat,
-                in1=mkj_grouped[:, jc * JC : (jc + 1) * JC, :]
-                .rearrange("p j t -> p (j t)")
-                .unsqueeze(1)
-                .to_broadcast([P, ND, JC * PACK]),
-                op=ALU.mult,
-            )
             b_codes = b_mx.tile([P, ND, JC], U32, align_bytes=64)
             b_scales = b_mx.tile([P, ND, JC], U8, align_bytes=64)
             nc.vector.quantize_mx(
                 out=b_codes[:].rearrange("p d j -> p (d j)").bitcast(FP8X4),
                 scales=b_scales[:].rearrange("p d j -> p (d j)"),
-                in_=b_grouped[:].rearrange("p d j t -> p (d j t)"),
+                in_=b_grouped_tiles[jc][:].rearrange("p d j t -> p (d j t)"),
             )
             quantised_b.append((b_codes, b_scales))
 
@@ -176,74 +203,77 @@ def tile_trianglemultiplicativeupdate_pa_kernel(
 
         def product(where, block, n, d, first, last):
             ip, jc = block
-            it = ip * PAIR + n
             b_codes, b_scales = quantised_b[jc]
+            i_cols = slice(n * P, (n + 1) * P)
             nc.tensor.matmul_mx(
                 out=where[:, n * JC : (n + 1) * JC],
-                lhsT=a_codes[:, it, d * P : (d + 1) * P].bitcast(FP8X4),
-                lhsT_scale=a_scales[:, it, d * P : (d + 1) * P],
+                lhsT=a_codes[:, ip, d, i_cols].bitcast(FP8X4),
+                lhsT_scale=a_scales[:, ip, d, i_cols],
                 rhs=b_codes[:, d, :].bitcast(FP8X4),
                 rhs_scale=b_scales[:, d, :],
                 start=first,
                 stop=last,
             )
 
-        def products_of_two_channels(block, q):
+        def product_T(where, block, d):
+            ip, jc = block
+            b_codes, b_scales = quantised_b[jc]
+            nc.tensor.matmul_mx(
+                out=where,
+                lhsT=b_codes[:, d, :].bitcast(FP8X4),
+                lhsT_scale=b_scales[:, d, :],
+                rhs=a_codes[:, ip, d, :].bitcast(FP8X4),
+                rhs_scale=a_scales[:, ip, d, :],
+                start=True,
+                stop=True,
+            )
+
+        def squares(m, q):
+            if q == 0:
+                squares_T = slabs.tile([P, ND, BLOCK], F32, tag="slab", align_bytes=64)
+                tiles_of[m].update(squares_T=squares_T)
             x_ps = psum.tile([P, 2, BLOCK], F32, tag="bank")
             for e in range(2):
-                for n in range(PAIR):
-                    product(x_ps[:, e, :], block, n, 2 * q + e, True, True)
-            return x_ps
+                product_T(x_ps[:, e, :], blocks[m], 2 * q + e)
+            nc.scalar.activation(
+                out=tiles_of[m]["squares_T"][:, 2 * q : 2 * q + 2, :], in_=x_ps[:], func=ACT.Square
+            )
 
-        def sums_and_squares(m):
-            sum_ps = psum.tile([P, BLOCK], F32, tag="bank")
-            for n in range(PAIR):
-                for d in range(ND):
-                    product(sum_ps, blocks[m], n, d, d == 0, d == ND - 1)
-            mean_sq = ln.tile([P, BLOCK], F32)
-            nc.scalar.activation(out=mean_sq[:], in_=sum_ps[:], func=ACT.Square, scale=1.0 / ND)
-            neg_mean = ln.tile([P, BLOCK], F32)
-            nc.scalar.activation(out=neg_mean[:], in_=sum_ps[:], func=ACT.Copy, scale=-1.0 / ND)
-            squares = planes.tile([P, ND, BLOCK], F32)
+        def every_square(m):
             for q in range(HALF):
-                x_ps = products_of_two_channels(blocks[m], q)
-                nc.scalar.activation(out=squares[:, 2 * q : 2 * q + 2, :], in_=x_ps[:], func=ACT.Square)
-            tiles_of[m].update(mean_sq=mean_sq, neg_mean=neg_mean, squares=squares)
+                squares(m, q)
 
-        def add_squares(m):
-            squares = tiles_of[m]["squares"]
-            sum_sq_T_ps = psum.tile([P, BLOCK], F32, tag="bank")
+        def sums(m):
+            squares_T = tiles_of[m]["squares_T"]
+            sums_ps = stats.tile([P, 2, BLOCK], F32)
             for n in range(PAIR):
                 cols = slice(n * JC, (n + 1) * JC)
                 for d in range(ND):
                     nc.tensor.matmul(
-                        out=sum_sq_T_ps[:, cols],
-                        lhsT=squares[:, d, cols],
+                        out=sums_ps[:, 0, cols],
+                        lhsT=squares_T[:, d, n * P : (n + 1) * P],
                         rhs=ident_f32[:],
                         is_transpose=True,
                         start=(d == 0),
                         stop=(d == ND - 1),
                     )
-            tiles_of[m].update(sum_sq_T_ps=sum_sq_T_ps)
-
-        def copy_sum_of_squares(m):
-            sum_sq_T = ln.tile([P, BLOCK], F32)
-            nc.scalar.copy(out=sum_sq_T[:], in_=tiles_of[m]["sum_sq_T_ps"][:])
-            tiles_of[m].update(sum_sq_T=sum_sq_T)
-
-        def transpose_sum_of_squares_back(m):
-            sum_sq_T = tiles_of[m]["sum_sq_T"]
-            sum_sq_ps = psum.tile([P, BLOCK], F32, tag="bank")
             for n in range(PAIR):
-                cols = slice(n * JC, (n + 1) * JC)
-                nc.tensor.transpose(sum_sq_ps[:, cols], sum_sq_T[:, cols], ident_f32[:])
-            tiles_of[m].update(sum_sq_ps=sum_sq_ps)
+                for d in range(ND):
+                    product(sums_ps[:, 1, :], blocks[m], n, d, d == 0, d == ND - 1)
+            tiles_of[m].update(sums_ps=sums_ps)
+
+        def mean_squared(m):
+            mean_sq = ln.tile([P, BLOCK], F32)
+            nc.scalar.activation(
+                out=mean_sq[:], in_=tiles_of[m]["sums_ps"][:, 1, :], func=ACT.Square, scale=1.0 / ND
+            )
+            tiles_of[m].update(mean_sq=mean_sq)
 
         def variance(m):
             var = ln.tile([P, BLOCK], F32)
             nc.vector.scalar_tensor_tensor(
                 out=var[:],
-                in0=tiles_of[m]["sum_sq_ps"][:],
+                in0=tiles_of[m]["sums_ps"][:, 0, :],
                 scalar=1.0 / ND,
                 in1=tiles_of[m]["mean_sq"][:],
                 op0=ALU.mult,
@@ -260,36 +290,47 @@ def tile_trianglemultiplicativeupdate_pa_kernel(
 
         def minus_mean_times_rstd(m):
             neg_mean_rstd = ln.tile([P, BLOCK], F32)
-            nc.vector.tensor_tensor(
-                out=neg_mean_rstd[:], in0=tiles_of[m]["neg_mean"][:], in1=tiles_of[m]["rstd"][:], op=ALU.mult
+            nc.vector.scalar_tensor_tensor(
+                out=neg_mean_rstd[:],
+                in0=tiles_of[m]["sums_ps"][:, 1, :],
+                scalar=-1.0 / ND,
+                in1=tiles_of[m]["rstd"][:],
+                op0=ALU.mult,
+                op1=ALU.mult,
             )
             tiles_of[m].update(neg_mean_rstd=neg_mean_rstd)
 
-        def shifts(m):
-            shift = planes.tile([P, ND, BLOCK], F32)
-            for d in range(HALF):
+        def shifts(m, part):
+            if part == 0:
+                shift = slabs.tile([P, ND, BLOCK], F32, tag="slab", align_bytes=64)
+                tiles_of[m].update(shift=shift)
+            middle = SHIFTS_ON_SCALAR // 2
+            for d in range(middle) if part == 0 else range(middle, SHIFTS_ON_SCALAR):
                 nc.scalar.activation(
-                    out=shift[:, d, :],
+                    out=tiles_of[m]["shift"][:, d, :],
                     in_=tiles_of[m]["neg_mean_rstd"][:],
                     func=ACT.Identity,
                     scale=w_col[:, d : d + 1],
                     bias=bias_col[:, d : d + 1],
                 )
-            for d in range(HALF, ND):
-                nc.vector.tensor_scalar(
-                    out=shift[:, d, :],
-                    in0=tiles_of[m]["neg_mean_rstd"][:],
-                    scalar1=w_col[:, d : d + 1],
-                    scalar2=bias_col[:, d : d + 1],
-                    op0=ALU.mult,
-                    op1=ALU.add,
-                )
-            tiles_of[m].update(shift=shift)
+
+        def shift_on_vector(m, d, cols):
+            nc.vector.tensor_scalar(
+                out=tiles_of[m]["shift"][:, d, cols],
+                in0=tiles_of[m]["neg_mean_rstd"][:, cols],
+                scalar1=w_col[:, d : d + 1],
+                scalar2=bias_col[:, d : d + 1],
+                op0=ALU.mult,
+                op1=ALU.add,
+            )
 
         def scale_products(m):
-            scaled = planes.tile([P, ND, BLOCK], F32, bufs=1)
+            scaled = slabs.tile([P, ND, BLOCK], F32, tag="slab", align_bytes=64)
             for q in range(HALF):
-                x_ps = products_of_two_channels(blocks[m], q)
+                x_ps = psum.tile([P, 2, BLOCK], F32, tag="bank")
+                for e in range(2):
+                    for n in range(PAIR):
+                        product(x_ps[:, e, :], blocks[m], n, 2 * q + e, True, True)
                 for e in range(2):
                     d = 2 * q + e
                     nc.vector.scalar_tensor_tensor(
@@ -304,51 +345,103 @@ def tile_trianglemultiplicativeupdate_pa_kernel(
 
         def add_shifts_and_store(m):
             ip, jc = blocks[m]
-            for n in range(PAIR):
-                cols = slice(n * JC, (n + 1) * JC)
-                result = results.tile([P, JC, ND], F32)
-                nc.vector.tensor_tensor(
-                    out=result[:].rearrange("p (c e) d -> p c d e", e=2),
-                    in0=tiles_of[m]["scaled"][:, :, cols].rearrange("p d (c e) -> p c d e", e=2),
-                    in1=tiles_of[m]["shift"][:, :, cols].rearrange("p d (c e) -> p c d e", e=2),
-                    op=ALU.add,
-                )
-                nc.sync.dma_start(
-                    out=out_rows[ip * PAIR + n, :, jc * JC * ND : (jc + 1) * JC * ND],
-                    in_=result[:].rearrange("p j d -> p (j d)"),
-                )
+            every = slice(0, BLOCK)
+            gpsimd_cols = slice(0, JC)
+            vector_cols = slice(JC, BLOCK)
+            shift_on_vector(m, ND - 1, vector_cols)
+            for d in range(SHIFTS_ON_SCALAR, ND - 1):
+                shift_on_vector(m, d, every)
+            add(m, nc.vector, 1)
+            shift_on_vector(m, ND - 1, gpsimd_cols)
+            add(m, nc.gpsimd, 0)
 
-        load_a(0)
-        load_a(1)
-        nc.sync.dma_start(out=mkj[:], in_=mkj_rows)
-        load_b(0)
-        load_a(2)
-        load_b(1)
-        load_b(2)
+        def add(m, engine, n):
+            ip, jc = blocks[m]
+            cols = slice(n * JC, (n + 1) * JC)
+            result = results.tile([P, JC, ND], F32)
+            engine.tensor_tensor(
+                out=result[:].rearrange("p (c e) d -> p c d e", e=2),
+                in0=tiles_of[m]["scaled"][:, :, cols].rearrange("p d (c e) -> p c d e", e=2),
+                in1=tiles_of[m]["shift"][:, :, cols].rearrange("p d (c e) -> p c d e", e=2),
+                op=ALU.add,
+            )
+            nc.sync.dma_start(
+                out=out_rows[ip * PAIR + n, :, jc * JC * ND : (jc + 1) * JC * ND],
+                in_=result[:].rearrange("p j d -> p (j d)"),
+            )
 
-        prepare_a_pair(0)
-        nc.scalar.copy(out=mkj_grouped[:], in_=mkj[:].rearrange("p t j -> p j t"))
-        regroup_b(0)
+        def group_mask_kj():
+            nc.scalar.copy(out=mkj_grouped[:], in_=mkj[:].rearrange("p t j -> p j t"))
+
+        def columns():
+            nc.vector.tensor_copy(out=w_col[:], in_=w_bf16[:])
+            nc.vector.tensor_copy(out=bias_col[:], in_=bias_bf16[:])
+
+        turn_mask(0, 0)
+        turn_a(0, 0)
+        regroup_b(0, 0)
+        group_mask_kj()
+        turn_mask(0, 1)
+        turn_a(0, 1, (0, 1))
+        regroup_b(0, 1)
         quantise_b(0)
-        prepare_a_pair(1)
-        for jc in range(1, J_CHUNKS):
-            regroup_b(jc)
-            quantise_b(jc)
-        nc.vector.tensor_copy(out=w_col[:], in_=w_bf16[:])
-        nc.vector.tensor_copy(out=bias_col[:], in_=bias_bf16[:])
+        mask_a(0, 0)
+        quantise_a(0, 0)
+        turn_a(0, 1, (2, 3))
+        turn_mask(1, 0)
+        turn_a(1, 0)
+        mask_a(0, 1)
+        quantise_a(0, 1)
+        turn_mask(1, 1)
+        turn_a(1, 1)
+        every_square(0)
+        columns()
+        mask_a(1, 0)
+        quantise_a(1, 0)
+        regroup_b(1, 0)
+        mask_a(1, 1)
+        quantise_a(1, 1)
+        regroup_b(1, 1)
+        sums(0)
+        mean_squared(0)
+        every_square(1)
+        mask_b(1)
+        variance(0)
+        quantise_b(1)
+        reciprocal_std(0)
+        regroup_b(3, 0)
+        sums(1)
+        mean_squared(1)
+        every_square(2)
+        regroup_b(2, 0)
+        minus_mean_times_rstd(0)
+        variance(1)
+        reciprocal_std(1)
+        regroup_b(3, 1)
+        shifts(0, 0)
+        shifts(0, 1)
+        sums(2)
+        mean_squared(2)
+        regroup_b(2, 1)
+        quantise_b(2)
+        every_square(3)
+        minus_mean_times_rstd(1)
+        mask_b(3)
+        variance(2)
+        quantise_b(3)
 
-        def stage(work, m):
-            if 0 <= m < len(blocks):
-                work(m)
+        def stage(work, m, *which):
+            if m < len(blocks):
+                work(m, *which)
 
-        for m in range(-4, len(blocks)):
+        for m in range(len(blocks)):
             stage(scale_products, m)
-            stage(add_squares, m + 2)
-            stage(copy_sum_of_squares, m + 2)
-            stage(minus_mean_times_rstd, m + 1)
-            stage(add_shifts_and_store, m)
-            stage(sums_and_squares, m + 4)
-            stage(transpose_sum_of_squares_back, m + 2)
-            stage(variance, m + 2)
+            stage(shifts, m + 1, 0)
             stage(reciprocal_std, m + 2)
-            stage(shifts, m + 1)
+            stage(shifts, m + 1, 1)
+            stage(sums, m + 3)
+            stage(mean_squared, m + 3)
+            stage(every_square, m + 4)
+            stage(minus_mean_times_rstd, m + 2)
+            stage(add_shifts_and_store, m)
+            stage(variance, m + 3)

@@ -26,10 +26,11 @@ I_PAIRS = I_TILES // PAIR
 BLOCK = PAIR * JC
 SLABS = 16
 EPS = 1e-5
-A_ON_SCALAR = ((0, 2), (0, 2), (0, 1, 2, 3), ())
+A_ON_SCALAR = ((0, 2), (0, 2), (0, 1, 2, 3), (0, 2))
 B_ON_VECTOR = (0, 2)
 B_ON_GPSIMD = ()
-SHIFTS_ON_SCALAR = 6
+LAST_PARTS = 2
+SHIFTS_ON_SCALAR = (6, 6, 6, 7, 7, 7, 7, 8)
 B_PARTS = 2
 
 FLOPS = 2 * NI * NJ * NK * ND
@@ -53,7 +54,7 @@ def tile_trianglemultiplicativeupdate_pa_kernel(
         slabs = ctx.enter_context(tc.tile_pool(name="slabs", bufs=SLABS))
         b_mx = ctx.enter_context(tc.tile_pool(name="b_mx", bufs=J_CHUNKS))
         ln = ctx.enter_context(tc.tile_pool(name="ln", bufs=3))
-        results = ctx.enter_context(tc.tile_pool(name="results", bufs=4))
+        results = ctx.enter_context(tc.tile_pool(name="results", bufs=6))
         psum = ctx.enter_context(tc.psum_pool(name="psum", bufs=6))
         stats = ctx.enter_context(tc.psum_pool(name="stats", bufs=2))
 
@@ -62,20 +63,29 @@ def tile_trianglemultiplicativeupdate_pa_kernel(
         a_raw_tiles = []
         b_raw_tiles = []
 
+        def load_mkj(first, last):
+            nc.sync.dma_start(out=mkj[:, :, first:last], in_=mkj_rows[:, :, first:last])
+
         def load_a(it):
             nc.sync.dma_start(out=mik[:, it, :], in_=mik_rows[:, it, :])
             a_raw = slabs.tile([P, NK * ND], BF16, tag="slab", align_bytes=64)
             nc.sync.dma_start(out=a_raw[:], in_=a_rows[it])
             a_raw_tiles.append(a_raw)
 
-        def load_b(jc):
-            b_raw = slabs.tile([P, PACK, JC * ND], BF16, tag="slab", align_bytes=64)
-            nc.sync.dma_start(out=b_raw[:], in_=b_rows[:, :, jc * JC * ND : (jc + 1) * JC * ND])
-            b_raw_tiles.append(b_raw)
+        def load_b(jc, first=0, last=JC):
+            if first == 0:
+                b_raw = slabs.tile([P, PACK, JC, ND], BF16, tag="slab", align_bytes=64)
+                b_raw_tiles.append(b_raw)
+            rows = b_rows[:, :, (jc * JC + first) * ND : (jc * JC + last) * ND]
+            nc.sync.dma_start(
+                out=b_raw_tiles[jc][:, :, first:last, :].rearrange("p t j d -> p t (j d)"), in_=rows
+            )
 
+        load_mkj(0, JC)
+        load_b(0, 0, JC // 2)
         load_a(0)
-        nc.sync.dma_start(out=mkj[:], in_=mkj_rows)
-        load_b(0)
+        load_b(0, JC // 2, JC)
+        load_mkj(JC, NJ)
         load_a(1)
         load_a(2)
         load_b(1)
@@ -161,15 +171,15 @@ def tile_trianglemultiplicativeupdate_pa_kernel(
                 in_=a_grouped_pairs[ip][h][:].rearrange("p d i t -> p (d i t)"),
             )
 
-        def regroup_b(jc, h):
-            if h == 0:
+        def regroup_b(jc, h, first=0, last=JC):
+            if jc not in b_grouped_tiles:
                 b_grouped = slabs.tile([P, ND, JC, PACK], BF16, tag="slab", align_bytes=64)
                 b_grouped_tiles[jc] = b_grouped
             half = slice(h * HALF, (h + 1) * HALF)
-            src = b_raw_tiles[jc][:].rearrange("p t (j d) -> p j t d", d=ND)[:, :, :, half]
-            dst = b_grouped_tiles[jc][:].rearrange("p d j t -> p j t d")[:, :, :, half]
-            mask = mkj[:, :, jc * JC : (jc + 1) * JC].rearrange("p t j -> p j t")
-            mask = mask.unsqueeze(3).to_broadcast([P, JC, PACK, HALF])
+            src = b_raw_tiles[jc][:].rearrange("p t j d -> p j t d")[:, first:last, :, half]
+            dst = b_grouped_tiles[jc][:].rearrange("p d j t -> p j t d")[:, first:last, :, half]
+            mask = mkj[:, :, jc * JC + first : jc * JC + last].rearrange("p t j -> p j t")
+            mask = mask.unsqueeze(3).to_broadcast([P, last - first, PACK, HALF])
             if jc in B_ON_VECTOR:
                 nc.vector.tensor_tensor(out=dst, in0=src, in1=mask, op=ALU.mult)
             elif jc in B_ON_GPSIMD:
@@ -304,8 +314,8 @@ def tile_trianglemultiplicativeupdate_pa_kernel(
             if part == 0:
                 shift = slabs.tile([P, ND, BLOCK], F32, tag="slab", align_bytes=64)
                 tiles_of[m].update(shift=shift)
-            middle = SHIFTS_ON_SCALAR // 2
-            for d in range(middle) if part == 0 else range(middle, SHIFTS_ON_SCALAR):
+            count = SHIFTS_ON_SCALAR[m]
+            for d in range(count // 2) if part == 0 else range(count // 2, count):
                 nc.scalar.activation(
                     out=tiles_of[m]["shift"][:, d, :],
                     in_=tiles_of[m]["neg_mean_rstd"][:],
@@ -344,46 +354,55 @@ def tile_trianglemultiplicativeupdate_pa_kernel(
             tiles_of[m].update(scaled=scaled)
 
         def add_shifts_and_store(m):
-            ip, jc = blocks[m]
             every = slice(0, BLOCK)
-            gpsimd_cols = slice(0, JC)
-            vector_cols = slice(JC, BLOCK)
-            shift_on_vector(m, ND - 1, vector_cols)
-            for d in range(SHIFTS_ON_SCALAR, ND - 1):
+            if m == len(blocks) - 1:
+                for d in range(SHIFTS_ON_SCALAR[m], ND):
+                    shift_on_vector(m, d, every)
+                for n in range(PAIR):
+                    add(m, nc.vector, n, LAST_PARTS)
+                return
+            shift_on_vector(m, ND - 1, slice(JC, BLOCK))
+            for d in range(SHIFTS_ON_SCALAR[m], ND - 1):
                 shift_on_vector(m, d, every)
-            add(m, nc.vector, 1)
-            shift_on_vector(m, ND - 1, gpsimd_cols)
-            add(m, nc.gpsimd, 0)
+            add(m, nc.vector, 1, 1)
+            shift_on_vector(m, ND - 1, slice(0, JC))
+            add(m, nc.gpsimd, 0, 1)
 
-        def add(m, engine, n):
+        def add(m, engine, n, parts):
             ip, jc = blocks[m]
-            cols = slice(n * JC, (n + 1) * JC)
-            result = results.tile([P, JC, ND], F32)
-            engine.tensor_tensor(
-                out=result[:].rearrange("p (c e) d -> p c d e", e=2),
-                in0=tiles_of[m]["scaled"][:, :, cols].rearrange("p d (c e) -> p c d e", e=2),
-                in1=tiles_of[m]["shift"][:, :, cols].rearrange("p d (c e) -> p c d e", e=2),
-                op=ALU.add,
-            )
-            nc.sync.dma_start(
-                out=out_rows[ip * PAIR + n, :, jc * JC * ND : (jc + 1) * JC * ND],
-                in_=result[:].rearrange("p j d -> p (j d)"),
-            )
+            width = JC // parts
+            for part in range(parts):
+                cols = slice(n * JC + part * width, n * JC + (part + 1) * width)
+                result = results.tile([P, width, ND], F32)
+                engine.tensor_tensor(
+                    out=result[:].rearrange("p (c e) d -> p c d e", e=2),
+                    in0=tiles_of[m]["scaled"][:, :, cols].rearrange("p d (c e) -> p c d e", e=2),
+                    in1=tiles_of[m]["shift"][:, :, cols].rearrange("p d (c e) -> p c d e", e=2),
+                    op=ALU.add,
+                )
+                first = (jc * JC + part * width) * ND
+                nc.sync.dma_start(
+                    out=out_rows[ip * PAIR + n, :, first : first + width * ND],
+                    in_=result[:].rearrange("p j d -> p (j d)"),
+                )
 
-        def group_mask_kj():
-            nc.scalar.copy(out=mkj_grouped[:], in_=mkj[:].rearrange("p t j -> p j t"))
+        def group_mask_kj(jc):
+            cols = slice(jc * JC, (jc + 1) * JC)
+            nc.scalar.copy(out=mkj_grouped[:, cols, :], in_=mkj[:, :, cols].rearrange("p t j -> p j t"))
 
         def columns():
             nc.vector.tensor_copy(out=w_col[:], in_=w_bf16[:])
             nc.vector.tensor_copy(out=bias_col[:], in_=bias_bf16[:])
 
+        regroup_b(0, 0, 0, JC // 2)
+        regroup_b(0, 1, 0, JC // 2)
         turn_mask(0, 0)
         turn_a(0, 0)
-        regroup_b(0, 0)
-        group_mask_kj()
+        group_mask_kj(1)
         turn_mask(0, 1)
+        regroup_b(0, 0, JC // 2)
         turn_a(0, 1, (0, 1))
-        regroup_b(0, 1)
+        regroup_b(0, 1, JC // 2)
         quantise_b(0)
         mask_a(0, 0)
         quantise_a(0, 0)
@@ -409,6 +428,7 @@ def tile_trianglemultiplicativeupdate_pa_kernel(
         variance(0)
         quantise_b(1)
         reciprocal_std(0)
+        group_mask_kj(3)
         regroup_b(3, 0)
         sums(1)
         mean_squared(1)
@@ -436,12 +456,12 @@ def tile_trianglemultiplicativeupdate_pa_kernel(
 
         for m in range(len(blocks)):
             stage(scale_products, m)
-            stage(shifts, m + 1, 0)
             stage(reciprocal_std, m + 2)
+            stage(shifts, m + 1, 0)
             stage(shifts, m + 1, 1)
             stage(sums, m + 3)
             stage(mean_squared, m + 3)
             stage(every_square, m + 4)
-            stage(minus_mean_times_rstd, m + 2)
             stage(add_shifts_and_store, m)
+            stage(minus_mean_times_rstd, m + 2)
             stage(variance, m + 3)

@@ -27,7 +27,7 @@ BLOCK = PAIR * JC
 SLABS = 16
 EPS = 1e-5
 A_ON_SCALAR = ((0, 2), (0, 2), (0, 1, 2, 3), (0, 2))
-B_ON_VECTOR = (0, 2)
+B_ON_VECTOR = ((0, 0), (0, 64), (2, 0))
 B_ON_GPSIMD = ()
 LAST_PARTS = 2
 SHIFTS_ON_SCALAR = (6, 6, 6, 7, 7, 7, 7, 8)
@@ -180,17 +180,18 @@ def tile_trianglemultiplicativeupdate_pa_kernel(
             dst = b_grouped_tiles[jc][:].rearrange("p d j t -> p j t d")[:, first:last, :, half]
             mask = mkj[:, :, jc * JC + first : jc * JC + last].rearrange("p t j -> p j t")
             mask = mask.unsqueeze(3).to_broadcast([P, last - first, PACK, HALF])
-            if jc in B_ON_VECTOR:
+            if (jc, first) in B_ON_VECTOR:
                 nc.vector.tensor_tensor(out=dst, in0=src, in1=mask, op=ALU.mult)
-            elif jc in B_ON_GPSIMD:
-                for c in range(0, JC, JC // B_PARTS):
-                    cols = slice(c, c + JC // B_PARTS)
+            elif (jc, first) in B_ON_GPSIMD:
+                step = JC // B_PARTS
+                for c in range(0, last - first, step):
+                    cols = slice(c, c + step)
                     nc.gpsimd.tensor_tensor(out=dst[:, cols], in0=src[:, cols], in1=mask[:, cols], op=ALU.mult)
             else:
                 nc.scalar.copy(out=dst, in_=src)
 
         def mask_b(jc):
-            if jc in B_ON_VECTOR or jc in B_ON_GPSIMD:
+            if (jc, 0) in B_ON_VECTOR or (jc, 0) in B_ON_GPSIMD:
                 return
             b_flat = b_grouped_tiles[jc][:].rearrange("p d j t -> p d (j t)")
             mask = mkj_grouped[:, jc * JC : (jc + 1) * JC, :].rearrange("p j t -> p (j t)")
@@ -355,15 +356,16 @@ def tile_trianglemultiplicativeupdate_pa_kernel(
 
         def add_shifts_and_store(m):
             every = slice(0, BLOCK)
-            if m == len(blocks) - 1:
-                for d in range(SHIFTS_ON_SCALAR[m], ND):
-                    shift_on_vector(m, d, every)
+            last = m == len(blocks) - 1
+            for d in range(SHIFTS_ON_SCALAR[m], ND if last else ND - 1):
+                shift_on_vector(m, d, every)
+            if last:
                 for n in range(PAIR):
                     add(m, nc.vector, n, LAST_PARTS)
                 return
             shift_on_vector(m, ND - 1, slice(JC, BLOCK))
-            for d in range(SHIFTS_ON_SCALAR[m], ND - 1):
-                shift_on_vector(m, d, every)
+            if m + 2 < len(blocks):
+                minus_mean_times_rstd(m + 2)
             add(m, nc.vector, 1, 1)
             shift_on_vector(m, ND - 1, slice(0, JC))
             add(m, nc.gpsimd, 0, 1)
@@ -391,8 +393,8 @@ def tile_trianglemultiplicativeupdate_pa_kernel(
             nc.scalar.copy(out=mkj_grouped[:, cols, :], in_=mkj[:, :, cols].rearrange("p t j -> p j t"))
 
         def columns():
-            nc.vector.tensor_copy(out=w_col[:], in_=w_bf16[:])
-            nc.vector.tensor_copy(out=bias_col[:], in_=bias_bf16[:])
+            nc.gpsimd.tensor_copy(out=w_col[:], in_=w_bf16[:])
+            nc.gpsimd.tensor_copy(out=bias_col[:], in_=bias_bf16[:])
 
         regroup_b(0, 0, 0, JC // 2)
         regroup_b(0, 1, 0, JC // 2)
@@ -401,25 +403,25 @@ def tile_trianglemultiplicativeupdate_pa_kernel(
         group_mask_kj(1)
         turn_mask(0, 1)
         regroup_b(0, 0, JC // 2)
-        turn_a(0, 1, (0, 1))
         regroup_b(0, 1, JC // 2)
+        turn_a(0, 1, (0, 1))
         quantise_b(0)
-        mask_a(0, 0)
-        quantise_a(0, 0)
         turn_a(0, 1, (2, 3))
+        mask_a(0, 0)
+        mask_a(0, 1)
+        quantise_a(0, 0)
+        quantise_a(0, 1)
         turn_mask(1, 0)
         turn_a(1, 0)
-        mask_a(0, 1)
-        quantise_a(0, 1)
         turn_mask(1, 1)
         turn_a(1, 1)
         every_square(0)
         columns()
         mask_a(1, 0)
-        quantise_a(1, 0)
-        regroup_b(1, 0)
         mask_a(1, 1)
+        quantise_a(1, 0)
         quantise_a(1, 1)
+        regroup_b(1, 0)
         regroup_b(1, 1)
         sums(0)
         mean_squared(0)
@@ -443,9 +445,9 @@ def tile_trianglemultiplicativeupdate_pa_kernel(
         sums(2)
         mean_squared(2)
         regroup_b(2, 1)
-        quantise_b(2)
         every_square(3)
         minus_mean_times_rstd(1)
+        quantise_b(2)
         mask_b(3)
         variance(2)
         quantise_b(3)
@@ -463,5 +465,4 @@ def tile_trianglemultiplicativeupdate_pa_kernel(
             stage(mean_squared, m + 3)
             stage(every_square, m + 4)
             stage(add_shifts_and_store, m)
-            stage(minus_mean_times_rstd, m + 2)
             stage(variance, m + 3)

@@ -68,13 +68,13 @@ def tile_trianglemultiplicativeupdate_pa_kernel(
 
         def load_a(it):
             nc.sync.dma_start(out=mik[:, it, :], in_=mik_rows[:, it, :])
-            a_raw = slabs.tile([P, NK * ND], BF16, tag="slab", align_bytes=64)
+            a_raw = slabs.tile([P, NK * ND], BF16, tag="slab", align_bytes=256)
             nc.sync.dma_start(out=a_raw[:], in_=a_rows[it])
             a_raw_tiles.append(a_raw)
 
         def load_b(jc, first=0, last=JC):
             if first == 0:
-                b_raw = slabs.tile([P, PACK, JC, ND], BF16, tag="slab", align_bytes=64)
+                b_raw = slabs.tile([P, PACK, JC, ND], BF16, tag="slab", align_bytes=256)
                 b_raw_tiles.append(b_raw)
             rows = b_rows[:, :, (jc * JC + first) * ND : (jc * JC + last) * ND]
             nc.sync.dma_start(
@@ -95,9 +95,9 @@ def tile_trianglemultiplicativeupdate_pa_kernel(
 
         eps_col = consts.tile([P, 1], F32)
         nc.vector.memset(eps_col[:], EPS)
-        ident_f32 = consts.tile([P, P], F32)
+        ident_f32 = consts.tile([P, P], F32, align_bytes=256)
         make_identity(nc, ident_f32[:])
-        ident_bf16 = consts.tile([P, P], BF16)
+        ident_bf16 = consts.tile([P, P], BF16, align_bytes=256)
         make_identity(nc, ident_bf16[:])
         w_bf16 = consts.tile([P, ND], BF16)
         nc.gpsimd.dma_start(out=w_bf16[:], in_=ln_out_w.partition_broadcast(P))
@@ -108,8 +108,8 @@ def tile_trianglemultiplicativeupdate_pa_kernel(
         table_col = consts.tile([P, 1], F32)
         nc.scalar.activation(out=table_col[:], in_=eps_col[:], func=ACT.Abs_reciprocal_sqrt)
 
-        a_codes = keep.tile([P, I_PAIRS, ND, PAIR * P], U32, align_bytes=64)
-        a_scales = keep.tile([P, I_PAIRS, ND, PAIR * P], U8, align_bytes=64)
+        a_codes = keep.tile([P, I_PAIRS, ND, PAIR * P], U32, align_bytes=256)
+        a_scales = keep.tile([P, I_PAIRS, ND, PAIR * P], U8, align_bytes=256)
         mikT = keep.tile([P, I_TILES, P, PACK], BF16)
         mkj_grouped = keep.tile([P, NJ, PACK], BF16)
         a_grouped_pairs = [[] for ip in range(I_PAIRS)]
@@ -131,7 +131,7 @@ def tile_trianglemultiplicativeupdate_pa_kernel(
             it = ip * PAIR + n
             if not a_grouped_pairs[ip]:
                 for h in range(2):
-                    a_half = slabs.tile([P, HALF, PAIR * P, PACK], BF16, tag="slab", align_bytes=64)
+                    a_half = slabs.tile([P, HALF, PAIR * P, PACK], BF16, tag="slab", align_bytes=256)
                     a_grouped_pairs[ip].append(a_half)
             a_words = a_raw_tiles[it][:].bitcast(F32).rearrange("p (k w) -> p k w", w=HALF)
             pair_mask = mikT[:, it, :, :].unsqueeze(1).to_broadcast([P, 2, P, PACK])
@@ -173,7 +173,7 @@ def tile_trianglemultiplicativeupdate_pa_kernel(
 
         def regroup_b(jc, h, first=0, last=JC):
             if jc not in b_grouped_tiles:
-                b_grouped = slabs.tile([P, ND, JC, PACK], BF16, tag="slab", align_bytes=64)
+                b_grouped = slabs.tile([P, ND, JC, PACK], BF16, tag="slab", align_bytes=256)
                 b_grouped_tiles[jc] = b_grouped
             half = slice(h * HALF, (h + 1) * HALF)
             src = b_raw_tiles[jc][:].rearrange("p t j d -> p j t d")[:, first:last, :, half]
@@ -200,8 +200,8 @@ def tile_trianglemultiplicativeupdate_pa_kernel(
             )
 
         def quantise_b(jc):
-            b_codes = b_mx.tile([P, ND, JC], U32, align_bytes=64)
-            b_scales = b_mx.tile([P, ND, JC], U8, align_bytes=64)
+            b_codes = b_mx.tile([P, ND, JC], U32, align_bytes=256)
+            b_scales = b_mx.tile([P, ND, JC], U8, align_bytes=256)
             nc.vector.quantize_mx(
                 out=b_codes[:].rearrange("p d j -> p (d j)").bitcast(FP8X4),
                 scales=b_scales[:].rearrange("p d j -> p (d j)"),
@@ -241,7 +241,7 @@ def tile_trianglemultiplicativeupdate_pa_kernel(
 
         def squares(m, q):
             if q == 0:
-                squares_T = slabs.tile([P, ND, BLOCK], F32, tag="slab", align_bytes=64)
+                squares_T = slabs.tile([P, ND, BLOCK], F32, tag="slab", align_bytes=256)
                 tiles_of[m].update(squares_T=squares_T)
             x_ps = psum.tile([P, 2, BLOCK], F32, tag="bank")
             for e in range(2):
@@ -274,14 +274,14 @@ def tile_trianglemultiplicativeupdate_pa_kernel(
             tiles_of[m].update(sums_ps=sums_ps)
 
         def mean_squared(m):
-            mean_sq = ln.tile([P, BLOCK], F32)
+            mean_sq = ln.tile([P, BLOCK], F32, align_bytes=256)
             nc.scalar.activation(
                 out=mean_sq[:], in_=tiles_of[m]["sums_ps"][:, 1, :], func=ACT.Square, scale=1.0 / ND
             )
             tiles_of[m].update(mean_sq=mean_sq)
 
         def variance(m):
-            var = ln.tile([P, BLOCK], F32)
+            var = ln.tile([P, BLOCK], F32, align_bytes=256)
             nc.vector.scalar_tensor_tensor(
                 out=var[:],
                 in0=tiles_of[m]["sums_ps"][:, 0, :],
@@ -293,14 +293,14 @@ def tile_trianglemultiplicativeupdate_pa_kernel(
             tiles_of[m].update(var=var)
 
         def reciprocal_std(m):
-            rstd = ln.tile([P, BLOCK], F32)
+            rstd = ln.tile([P, BLOCK], F32, align_bytes=256)
             nc.scalar.activation(
                 out=rstd[:], in_=tiles_of[m]["var"][:], func=ACT.Abs_reciprocal_sqrt, bias=eps_col[:, 0:1]
             )
             tiles_of[m].update(rstd=rstd)
 
         def minus_mean_times_rstd(m):
-            neg_mean_rstd = ln.tile([P, BLOCK], F32)
+            neg_mean_rstd = ln.tile([P, BLOCK], F32, align_bytes=256)
             nc.vector.scalar_tensor_tensor(
                 out=neg_mean_rstd[:],
                 in0=tiles_of[m]["sums_ps"][:, 1, :],
@@ -313,7 +313,7 @@ def tile_trianglemultiplicativeupdate_pa_kernel(
 
         def shifts(m, part):
             if part == 0:
-                shift = slabs.tile([P, ND, BLOCK], F32, tag="slab", align_bytes=64)
+                shift = slabs.tile([P, ND, BLOCK], F32, tag="slab", align_bytes=256)
                 tiles_of[m].update(shift=shift)
             count = SHIFTS_ON_SCALAR[m]
             for d in range(count // 2) if part == 0 else range(count // 2, count):
@@ -336,7 +336,7 @@ def tile_trianglemultiplicativeupdate_pa_kernel(
             )
 
         def scale_products(m):
-            scaled = slabs.tile([P, ND, BLOCK], F32, tag="slab", align_bytes=64)
+            scaled = slabs.tile([P, ND, BLOCK], F32, tag="slab", align_bytes=256)
             for q in range(HALF):
                 x_ps = psum.tile([P, 2, BLOCK], F32, tag="bank")
                 for e in range(2):

@@ -376,10 +376,11 @@ def tile_trianglemultiplicativeupdate_pa_kernel(
             for part in range(parts):
                 cols = slice(n * JC + part * width, n * JC + (part + 1) * width)
                 result = results.tile([P, width, ND], F32)
+                run = 4 if engine == nc.gpsimd else 2
                 engine.tensor_tensor(
-                    out=result[:].rearrange("p (c e) d -> p c d e", e=2),
-                    in0=tiles_of[m]["scaled"][:, :, cols].rearrange("p d (c e) -> p c d e", e=2),
-                    in1=tiles_of[m]["shift"][:, :, cols].rearrange("p d (c e) -> p c d e", e=2),
+                    out=result[:].rearrange("p (c e) d -> p c d e", e=run),
+                    in0=tiles_of[m]["scaled"][:, :, cols].rearrange("p d (c e) -> p c d e", e=run),
+                    in1=tiles_of[m]["shift"][:, :, cols].rearrange("p d (c e) -> p c d e", e=run),
                     op=ALU.add,
                 )
                 first = (jc * JC + part * width) * ND

@@ -122,10 +122,14 @@ def tile_trianglemultiplicativeupdate_pa_kernel(
 
         def turn_mask(ip, n):
             it = ip * PAIR + n
-            maskT_ps = psum.tile([P, PACK, P], BF16, tag="bank")
-            for t in range(PACK):
-                nc.tensor.transpose(maskT_ps[:, t, :], mik[:, it, t:NK:PACK], ident_bf16[:])
-            nc.scalar.copy(out=mikT[:, it, :, :], in_=maskT_ps[:].rearrange("p t i -> p i t"))
+            mask_words = mik[:, it, :].bitcast(F32)
+            maskT_ps = psum.tile([P, 2, P], F32, tag="bank")
+            for u in range(2):
+                nc.tensor.transpose(maskT_ps[:, u, :], mask_words[:, u : NK // 2 : 2], ident_f32[:])
+            nc.scalar.copy(
+                out=mikT[:, it, :, :].rearrange("p i t -> p (i t)").bitcast(F32).rearrange("p (i u) -> p i u", u=2),
+                in_=maskT_ps[:].rearrange("p u i -> p i u"),
+            )
 
         def turn_a(ip, n, ws=range(HALF)):
             it = ip * PAIR + n
@@ -254,9 +258,9 @@ def tile_trianglemultiplicativeupdate_pa_kernel(
             for q in range(HALF):
                 squares(m, q)
 
-        def sums(m):
+        def sum_squares(m):
             squares_T = tiles_of[m]["squares_T"]
-            sums_ps = stats.tile([P, 2, BLOCK], F32)
+            sums_ps = tiles_of[m]["sums_ps"]
             for n in range(PAIR):
                 cols = slice(n * JC, (n + 1) * JC)
                 for d in range(ND):
@@ -268,10 +272,17 @@ def tile_trianglemultiplicativeupdate_pa_kernel(
                         start=(d == 0),
                         stop=(d == ND - 1),
                     )
+
+        def sum_products(m):
+            sums_ps = stats.tile([P, 2, BLOCK], F32)
+            tiles_of[m].update(sums_ps=sums_ps)
             for n in range(PAIR):
                 for d in range(ND):
                     product(sums_ps[:, 1, :], blocks[m], n, d, d == 0, d == ND - 1)
-            tiles_of[m].update(sums_ps=sums_ps)
+
+        def sums(m):
+            sum_products(m)
+            sum_squares(m)
 
         def mean_squared(m):
             mean_sq = ln.tile([P, BLOCK], F32, align_bytes=256)
@@ -354,18 +365,18 @@ def tile_trianglemultiplicativeupdate_pa_kernel(
                     )
             tiles_of[m].update(scaled=scaled)
 
-        def add_shifts_and_store(m):
-            every = slice(0, BLOCK)
+        def shifts_on_vector(m):
             last = m == len(blocks) - 1
             for d in range(SHIFTS_ON_SCALAR[m], ND if last else ND - 1):
-                shift_on_vector(m, d, every)
-            if last:
+                shift_on_vector(m, d, slice(0, BLOCK))
+            if not last:
+                shift_on_vector(m, ND - 1, slice(JC, BLOCK))
+
+        def add_shifts_and_store(m):
+            if m == len(blocks) - 1:
                 for n in range(PAIR):
                     add(m, nc.vector, n, LAST_PARTS)
                 return
-            shift_on_vector(m, ND - 1, slice(JC, BLOCK))
-            if m + 2 < len(blocks):
-                minus_mean_times_rstd(m + 2)
             add(m, nc.vector, 1, 1)
             shift_on_vector(m, ND - 1, slice(0, JC))
             add(m, nc.gpsimd, 0, 1)
@@ -391,7 +402,14 @@ def tile_trianglemultiplicativeupdate_pa_kernel(
 
         def group_mask_kj(jc):
             cols = slice(jc * JC, (jc + 1) * JC)
-            nc.scalar.copy(out=mkj_grouped[:, cols, :], in_=mkj[:, :, cols].rearrange("p t j -> p j t"))
+            nc.gpsimd.tensor_scalar(
+                out=mkj_grouped[:, cols, :],
+                in0=mkj[:, :, cols].rearrange("p t j -> p j t"),
+                scalar1=1.0,
+                scalar2=0.0,
+                op0=ALU.mult,
+                op1=ALU.add,
+            )
 
         def columns():
             nc.gpsimd.tensor_copy(out=w_col[:], in_=w_bf16[:])
@@ -424,7 +442,8 @@ def tile_trianglemultiplicativeupdate_pa_kernel(
         quantise_a(1, 1)
         regroup_b(1, 0)
         regroup_b(1, 1)
-        sums(0)
+        sum_products(0)
+        sum_squares(0)
         mean_squared(0)
         every_square(1)
         mask_b(1)
@@ -433,7 +452,8 @@ def tile_trianglemultiplicativeupdate_pa_kernel(
         reciprocal_std(0)
         group_mask_kj(3)
         regroup_b(3, 0)
-        sums(1)
+        sum_products(1)
+        sum_squares(1)
         mean_squared(1)
         every_square(2)
         regroup_b(2, 0)
@@ -443,7 +463,8 @@ def tile_trianglemultiplicativeupdate_pa_kernel(
         regroup_b(3, 1)
         shifts(0, 0)
         shifts(0, 1)
-        sums(2)
+        sum_products(2)
+        sum_squares(2)
         mean_squared(2)
         regroup_b(2, 1)
         every_square(3)
@@ -452,6 +473,7 @@ def tile_trianglemultiplicativeupdate_pa_kernel(
         mask_b(3)
         variance(2)
         quantise_b(3)
+
 
         def stage(work, m, *which):
             if m < len(blocks):
@@ -462,8 +484,13 @@ def tile_trianglemultiplicativeupdate_pa_kernel(
             stage(reciprocal_std, m + 2)
             stage(shifts, m + 1, 0)
             stage(shifts, m + 1, 1)
-            stage(sums, m + 3)
+            stage(sum_products, m + 3)
+            stage(sum_squares, m + 3)
             stage(mean_squared, m + 3)
             stage(every_square, m + 4)
-            stage(add_shifts_and_store, m)
+            if m == 0:
+                shifts_on_vector(m)
+            stage(minus_mean_times_rstd, m + 2)
+            stage(shifts_on_vector, m + 1)
+            add_shifts_and_store(m)
             stage(variance, m + 3)

@@ -30,6 +30,7 @@ A_ON_SCALAR = ((0, 2), (0, 2), (0, 1, 2, 3), (0, 2))
 B_ON_VECTOR = ((0, 0), (0, 64), (2, 0))
 B_ON_GPSIMD = ()
 LAST_PARTS = 2
+RUN = 4
 SHIFTS_ON_SCALAR = (6, 6, 6, 7, 7, 7, 7, 8)
 B_PARTS = 2
 
@@ -324,13 +325,13 @@ def tile_trianglemultiplicativeupdate_pa_kernel(
 
         def shifts(m, part):
             if part == 0:
-                shift = slabs.tile([P, ND, BLOCK], F32, tag="slab", align_bytes=256)
+                shift = slabs.tile([P, BLOCK // RUN, ND, RUN], F32, tag="slab", align_bytes=256)
                 tiles_of[m].update(shift=shift)
             count = SHIFTS_ON_SCALAR[m]
             for d in range(count // 2) if part == 0 else range(count // 2, count):
                 nc.scalar.activation(
-                    out=tiles_of[m]["shift"][:, d, :],
-                    in_=tiles_of[m]["neg_mean_rstd"][:],
+                    out=tiles_of[m]["shift"][:, :, d, :],
+                    in_=tiles_of[m]["neg_mean_rstd"][:].rearrange("p (c i) -> p c i", i=RUN),
                     func=ACT.Identity,
                     scale=w_col[:, d : d + 1],
                     bias=bias_col[:, d : d + 1],
@@ -338,8 +339,8 @@ def tile_trianglemultiplicativeupdate_pa_kernel(
 
         def shift_on_vector(m, d, cols):
             nc.vector.tensor_scalar(
-                out=tiles_of[m]["shift"][:, d, cols],
-                in0=tiles_of[m]["neg_mean_rstd"][:, cols],
+                out=tiles_of[m]["shift"][:, cols.start // RUN : cols.stop // RUN, d, :],
+                in0=tiles_of[m]["neg_mean_rstd"][:, cols].rearrange("p (c i) -> p c i", i=RUN),
                 scalar1=w_col[:, d : d + 1],
                 scalar2=bias_col[:, d : d + 1],
                 op0=ALU.mult,
@@ -347,7 +348,7 @@ def tile_trianglemultiplicativeupdate_pa_kernel(
             )
 
         def scale_products(m):
-            scaled = slabs.tile([P, ND, BLOCK], F32, tag="slab", align_bytes=256)
+            scaled = slabs.tile([P, BLOCK // RUN, ND, RUN], F32, tag="slab", align_bytes=256)
             for q in range(HALF):
                 x_ps = psum.tile([P, 2, BLOCK], F32, tag="bank")
                 for e in range(2):
@@ -356,10 +357,10 @@ def tile_trianglemultiplicativeupdate_pa_kernel(
                 for e in range(2):
                     d = 2 * q + e
                     nc.vector.scalar_tensor_tensor(
-                        out=scaled[:, d, :],
-                        in0=x_ps[:, e, :],
+                        out=scaled[:, :, d, :],
+                        in0=x_ps[:, e, :].rearrange("p (c i) -> p c i", i=RUN),
                         scalar=w_col[:, d : d + 1],
-                        in1=tiles_of[m]["rstd"][:],
+                        in1=tiles_of[m]["rstd"][:].rearrange("p (c i) -> p c i", i=RUN),
                         op0=ALU.mult,
                         op1=ALU.mult,
                     )
@@ -385,13 +386,13 @@ def tile_trianglemultiplicativeupdate_pa_kernel(
             ip, jc = blocks[m]
             width = JC // parts
             for part in range(parts):
-                cols = slice(n * JC + part * width, n * JC + (part + 1) * width)
+                first = n * JC + part * width
+                groups = slice(first // RUN, (first + width) // RUN)
                 result = results.tile([P, width, ND], F32)
-                run = 4 if engine == nc.gpsimd else 2
                 engine.tensor_tensor(
-                    out=result[:].rearrange("p (c e) d -> p c d e", e=run),
-                    in0=tiles_of[m]["scaled"][:, :, cols].rearrange("p d (c e) -> p c d e", e=run),
-                    in1=tiles_of[m]["shift"][:, :, cols].rearrange("p d (c e) -> p c d e", e=run),
+                    out=result[:].rearrange("p (c i) d -> p c d i", i=RUN),
+                    in0=tiles_of[m]["scaled"][:, groups, :, :],
+                    in1=tiles_of[m]["shift"][:, groups, :, :],
                     op=ALU.add,
                 )
                 first = (jc * JC + part * width) * ND

@@ -101,9 +101,9 @@ def tile_trianglemultiplicativeupdate_pa_kernel(
         ident_bf16 = consts.tile([P, P], BF16, align_bytes=256)
         make_identity(nc, ident_bf16[:])
         w_bf16 = consts.tile([P, ND], BF16)
-        nc.gpsimd.dma_start(out=w_bf16[:], in_=ln_out_w.partition_broadcast(P))
+        nc.sync.dma_start(out=w_bf16[:], in_=ln_out_w.partition_broadcast(P))
         bias_bf16 = consts.tile([P, ND], BF16)
-        nc.gpsimd.dma_start(out=bias_bf16[:], in_=ln_out_b.partition_broadcast(P))
+        nc.sync.dma_start(out=bias_bf16[:], in_=ln_out_b.partition_broadcast(P))
         w_col = consts.tile([P, ND], F32)
         bias_col = consts.tile([P, ND], F32)
         table_col = consts.tile([P, 1], F32)

@@ -31,7 +31,7 @@ B_ON_VECTOR = ((0, 0), (0, 64), (2, 0))
 B_ON_GPSIMD = ()
 LAST_PARTS = 2
 RUN = 4
-SHIFTS_ON_SCALAR = (6, 6, 6, 7, 7, 7, 7, 8)
+SHIFTS_ON_SCALAR = (6, 6, 7, 7, 7, 7, 7, 8)
 B_PARTS = 2
 
 FLOPS = 2 * NI * NJ * NK * ND
@@ -89,8 +89,8 @@ def tile_trianglemultiplicativeupdate_pa_kernel(
         load_mkj(JC, NJ)
         load_a(1)
         load_a(2)
-        load_b(1)
         load_a(3)
+        load_b(1)
         load_b(2)
         load_b(3)
 
@@ -98,8 +98,6 @@ def tile_trianglemultiplicativeupdate_pa_kernel(
         nc.vector.memset(eps_col[:], EPS)
         ident_f32 = consts.tile([P, P], F32, align_bytes=256)
         make_identity(nc, ident_f32[:])
-        ident_bf16 = consts.tile([P, P], BF16, align_bytes=256)
-        make_identity(nc, ident_bf16[:])
         w_bf16 = consts.tile([P, ND], BF16)
         nc.sync.dma_start(out=w_bf16[:], in_=ln_out_w.partition_broadcast(P))
         bias_bf16 = consts.tile([P, ND], BF16)
@@ -421,6 +419,7 @@ def tile_trianglemultiplicativeupdate_pa_kernel(
         turn_mask(0, 0)
         turn_a(0, 0)
         group_mask_kj(1)
+        group_mask_kj(3)
         turn_mask(0, 1)
         regroup_b(0, 0, JC // 2)
         regroup_b(0, 1, JC // 2)
@@ -451,7 +450,6 @@ def tile_trianglemultiplicativeupdate_pa_kernel(
         variance(0)
         quantise_b(1)
         reciprocal_std(0)
-        group_mask_kj(3)
         regroup_b(3, 0)
         sum_products(1)
         sum_squares(1)

@@ -27,12 +27,11 @@ BLOCK = PAIR * JC
 SLABS = 16
 EPS = 1e-5
 A_ON_SCALAR = ((0, 2), (0, 2), (0, 1, 2, 3), (0, 2))
-B_ON_VECTOR = ((0, 0), (0, 64), (2, 0))
-B_ON_GPSIMD = ()
+B_ON_VECTOR = ((0, 0), (2, 0), (2, 1))
 LAST_PARTS = 2
+GPSIMD_COLUMNS = 144
 RUN = 4
 SHIFTS_ON_SCALAR = (6, 6, 7, 7, 7, 7, 7, 8)
-B_PARTS = 2
 
 FLOPS = 2 * NI * NJ * NK * ND
 
@@ -82,11 +81,11 @@ def tile_trianglemultiplicativeupdate_pa_kernel(
                 out=b_raw_tiles[jc][:, :, first:last, :].rearrange("p t j d -> p t (j d)"), in_=rows
             )
 
-        load_mkj(0, JC)
+        load_mkj(0, 2 * JC)
         load_b(0, 0, JC // 2)
         load_a(0)
         load_b(0, JC // 2, JC)
-        load_mkj(JC, NJ)
+        load_mkj(2 * JC, NJ)
         load_a(1)
         load_a(2)
         load_a(3)
@@ -183,23 +182,20 @@ def tile_trianglemultiplicativeupdate_pa_kernel(
             dst = b_grouped_tiles[jc][:].rearrange("p d j t -> p j t d")[:, first:last, :, half]
             mask = mkj[:, :, jc * JC + first : jc * JC + last].rearrange("p t j -> p j t")
             mask = mask.unsqueeze(3).to_broadcast([P, last - first, PACK, HALF])
-            if (jc, first) in B_ON_VECTOR:
+            if (jc, h) in B_ON_VECTOR:
                 nc.vector.tensor_tensor(out=dst, in0=src, in1=mask, op=ALU.mult)
-            elif (jc, first) in B_ON_GPSIMD:
-                step = JC // B_PARTS
-                for c in range(0, last - first, step):
-                    cols = slice(c, c + step)
-                    nc.gpsimd.tensor_tensor(out=dst[:, cols], in0=src[:, cols], in1=mask[:, cols], op=ALU.mult)
             else:
                 nc.scalar.copy(out=dst, in_=src)
 
-        def mask_b(jc):
-            if (jc, 0) in B_ON_VECTOR or (jc, 0) in B_ON_GPSIMD:
-                return
-            b_flat = b_grouped_tiles[jc][:].rearrange("p d j t -> p d (j t)")
-            mask = mkj_grouped[:, jc * JC : (jc + 1) * JC, :].rearrange("p j t -> p (j t)")
+        def mask_b(jc, hs=(0, 1), first=0, last=JC):
+            ds = slice(hs[0] * HALF, (hs[-1] + 1) * HALF)
+            b_flat = b_grouped_tiles[jc][:, ds, first:last, :].rearrange("p d j t -> p d (j t)")
+            mask = mkj_grouped[:, jc * JC + first : jc * JC + last, :].rearrange("p j t -> p (j t)")
             nc.vector.tensor_tensor(
-                out=b_flat, in0=b_flat, in1=mask.unsqueeze(1).to_broadcast([P, ND, JC * PACK]), op=ALU.mult
+                out=b_flat,
+                in0=b_flat,
+                in1=mask.unsqueeze(1).to_broadcast([P, len(hs) * HALF, (last - first) * PACK]),
+                op=ALU.mult,
             )
 
         def quantise_b(jc):
@@ -369,34 +365,34 @@ def tile_trianglemultiplicativeupdate_pa_kernel(
             for d in range(SHIFTS_ON_SCALAR[m], ND if last else ND - 1):
                 shift_on_vector(m, d, slice(0, BLOCK))
             if not last:
-                shift_on_vector(m, ND - 1, slice(JC, BLOCK))
+                shift_on_vector(m, ND - 1, slice(GPSIMD_COLUMNS, BLOCK))
 
         def add_shifts_and_store(m):
             if m == len(blocks) - 1:
-                for n in range(PAIR):
-                    add(m, nc.vector, n, LAST_PARTS)
+                width = JC // LAST_PARTS
+                for first in range(0, BLOCK, width):
+                    add(m, nc.vector, first, first + width)
                 return
-            add(m, nc.vector, 1, 1)
-            shift_on_vector(m, ND - 1, slice(0, JC))
-            add(m, nc.gpsimd, 0, 1)
+            add(m, nc.vector, GPSIMD_COLUMNS, BLOCK)
+            shift_on_vector(m, ND - 1, slice(0, GPSIMD_COLUMNS))
+            add(m, nc.gpsimd, 0, GPSIMD_COLUMNS)
 
-        def add(m, engine, n, parts):
+        def add(m, engine, first, last):
             ip, jc = blocks[m]
-            width = JC // parts
-            for part in range(parts):
-                first = n * JC + part * width
-                groups = slice(first // RUN, (first + width) // RUN)
-                result = results.tile([P, width, ND], F32)
-                engine.tensor_tensor(
-                    out=result[:].rearrange("p (c i) d -> p c d i", i=RUN),
-                    in0=tiles_of[m]["scaled"][:, groups, :, :],
-                    in1=tiles_of[m]["shift"][:, groups, :, :],
-                    op=ALU.add,
-                )
-                first = (jc * JC + part * width) * ND
+            groups = slice(first // RUN, last // RUN)
+            result = results.tile([P, last - first, ND], F32)
+            engine.tensor_tensor(
+                out=result[:].rearrange("p (c i) d -> p c d i", i=RUN),
+                in0=tiles_of[m]["scaled"][:, groups, :, :],
+                in1=tiles_of[m]["shift"][:, groups, :, :],
+                op=ALU.add,
+            )
+            for n in range(first // JC, (last - 1) // JC + 1):
+                start, end = max(first, n * JC), min(last, (n + 1) * JC)
+                at = (jc * JC + start - n * JC) * ND
                 nc.sync.dma_start(
-                    out=out_rows[ip * PAIR + n, :, first : first + width * ND],
-                    in_=result[:].rearrange("p j d -> p (j d)"),
+                    out=out_rows[ip * PAIR + n, :, at : at + (end - start) * ND],
+                    in_=result[:, start - first : end - first, :].rearrange("p j d -> p (j d)"),
                 )
 
         def group_mask_kj(jc):
@@ -414,15 +410,18 @@ def tile_trianglemultiplicativeupdate_pa_kernel(
             nc.gpsimd.tensor_copy(out=w_col[:], in_=w_bf16[:])
             nc.gpsimd.tensor_copy(out=bias_col[:], in_=bias_bf16[:])
 
+        group_mask_kj(0)
+        group_mask_kj(1)
         regroup_b(0, 0, 0, JC // 2)
         regroup_b(0, 1, 0, JC // 2)
+        mask_b(0, (1,), 0, JC // 2)
         turn_mask(0, 0)
+        regroup_b(0, 0, JC // 2)
         turn_a(0, 0)
-        group_mask_kj(1)
         group_mask_kj(3)
         turn_mask(0, 1)
-        regroup_b(0, 0, JC // 2)
         regroup_b(0, 1, JC // 2)
+        mask_b(0, (1,), JC // 2, JC)
         turn_a(0, 1, (0, 1))
         quantise_b(0)
         turn_a(0, 1, (2, 3))

@@ -26,8 +26,8 @@ I_PAIRS = I_TILES // PAIR
 BLOCK = PAIR * JC
 SLABS = 16
 EPS = 1e-5
-A_ON_SCALAR = ((0, 2), (0, 2), (0, 1, 2, 3), (0, 2))
-B_ON_VECTOR = ((0, 0), (2, 0), (2, 1))
+A_ON_SCALAR = ((0, 2), (0, 2), (0, 1, 2, 3), (0,))
+B_ON_VECTOR = ((0, 0), (2, 0), (2, 1), (3, 1))
 LAST_PARTS = 2
 GPSIMD_COLUMNS = 144
 RUN = 4
@@ -458,7 +458,6 @@ def tile_trianglemultiplicativeupdate_pa_kernel(
         minus_mean_times_rstd(0)
         variance(1)
         reciprocal_std(1)
-        regroup_b(3, 1)
         shifts(0, 0)
         shifts(0, 1)
         sum_products(2)
@@ -468,7 +467,8 @@ def tile_trianglemultiplicativeupdate_pa_kernel(
         every_square(3)
         minus_mean_times_rstd(1)
         quantise_b(2)
-        mask_b(3)
+        regroup_b(3, 1)
+        mask_b(3, (0,))
         variance(2)
         quantise_b(3)
 

from contextlib import ExitStack

import concourse.mybir as mybir
from concourse.masks import make_identity

FP8X4 = mybir.dt.float8_e4m3fn_x4
BF16 = mybir.dt.bfloat16
F32 = mybir.dt.float32
U32 = mybir.dt.uint32
U8 = mybir.dt.uint8
ALU = mybir.AluOpType
ACT = mybir.ActivationFunctionType

P = 128
PACK = 4
NI = 512
NK = P * PACK
NJ = 512
ND = 8
HALF = ND // 2
I_TILES = NI // P
JC = 128
J_CHUNKS = NJ // JC
PAIR = 2
I_PAIRS = I_TILES // PAIR
BLOCK = PAIR * JC
SLABS = 16
EPS = 1e-5
A_ON_SCALAR = ((0, 2), (0, 2), (0, 1, 2, 3), (0,))
B_ON_VECTOR = ((0, 0), (2, 0), (2, 1), (3, 1))
LAST_PARTS = 2
GPSIMD_COLUMNS = 144
RUN = 4
SHIFTS_ON_SCALAR = (6, 6, 7, 7, 7, 7, 7, 8)

FLOPS = 2 * NI * NJ * NK * ND


def tile_trianglemultiplicativeupdate_pa_kernel(
    tc, a_gated, b_gated, mask_ik, mask_kj, ln_out_w, ln_out_b, out
):
    nc = tc.nc

    a_rows = a_gated.rearrange("b (n p) k d -> (b n) p (k d)", p=P)
    mik_rows = mask_ik.rearrange("b (n p) k -> p (b n) k", p=P)
    b_rows = b_gated.rearrange("b (p t) j d -> p (b t) (j d)", t=PACK)
    mkj_rows = mask_kj.rearrange("b (p t) j -> p (b t) j", t=PACK)
    out_rows = out.rearrange("b (n p) j d -> (b n) p (j d)", p=P)

    with ExitStack() as ctx:
        ctx.enter_context(tc.manual_schedule())
        consts = ctx.enter_context(tc.tile_pool(name="consts", bufs=1))
        keep = ctx.enter_context(tc.tile_pool(name="keep", bufs=1))
        slabs = ctx.enter_context(tc.tile_pool(name="slabs", bufs=SLABS))
        b_mx = ctx.enter_context(tc.tile_pool(name="b_mx", bufs=J_CHUNKS))
        ln = ctx.enter_context(tc.tile_pool(name="ln", bufs=3))
        results = ctx.enter_context(tc.tile_pool(name="results", bufs=6))
        psum = ctx.enter_context(tc.psum_pool(name="psum", bufs=6))
        stats = ctx.enter_context(tc.psum_pool(name="stats", bufs=2))

        mik = keep.tile([P, I_TILES, NK], BF16)
        mkj = keep.tile([P, PACK, NJ], BF16)
        a_raw_tiles = []
        b_raw_tiles = []

        def load_mkj(first, last):
            nc.sync.dma_start(out=mkj[:, :, first:last], in_=mkj_rows[:, :, first:last])

        def load_a(it):
            nc.sync.dma_start(out=mik[:, it, :], in_=mik_rows[:, it, :])
            a_raw = slabs.tile([P, NK * ND], BF16, tag="slab", align_bytes=256)
            nc.sync.dma_start(out=a_raw[:], in_=a_rows[it])
            a_raw_tiles.append(a_raw)

        def load_b(jc, first=0, last=JC):
            if first == 0:
                b_raw = slabs.tile([P, PACK, JC, ND], BF16, tag="slab", align_bytes=256)
                b_raw_tiles.append(b_raw)
            rows = b_rows[:, :, (jc * JC + first) * ND : (jc * JC + last) * ND]
            nc.sync.dma_start(
                out=b_raw_tiles[jc][:, :, first:last, :].rearrange("p t j d -> p t (j d)"), in_=rows
            )

        load_mkj(0, 2 * JC)
        load_b(0, 0, JC // 2)
        load_a(0)
        load_b(0, JC // 2, JC)
        load_mkj(2 * JC, NJ)
        load_a(1)
        load_a(2)
        load_a(3)
        load_b(1)
        load_b(2)
        load_b(3)

        eps_col = consts.tile([P, 1], F32)
        nc.vector.memset(eps_col[:], EPS)
        ident_f32 = consts.tile([P, P], F32, align_bytes=256)
        make_identity(nc, ident_f32[:])
        w_bf16 = consts.tile([P, ND], BF16)
        nc.sync.dma_start(out=w_bf16[:], in_=ln_out_w.partition_broadcast(P))
        bias_bf16 = consts.tile([P, ND], BF16)
        nc.sync.dma_start(out=bias_bf16[:], in_=ln_out_b.partition_broadcast(P))
        w_col = consts.tile([P, ND], F32)
        bias_col = consts.tile([P, ND], F32)
        table_col = consts.tile([P, 1], F32)
        nc.scalar.activation(out=table_col[:], in_=eps_col[:], func=ACT.Abs_reciprocal_sqrt)

        a_codes = keep.tile([P, I_PAIRS, ND, PAIR * P], U32, align_bytes=256)
        a_scales = keep.tile([P, I_PAIRS, ND, PAIR * P], U8, align_bytes=256)
        mikT = keep.tile([P, I_TILES, P, PACK], BF16)
        mkj_grouped = keep.tile([P, NJ, PACK], BF16)
        a_grouped_pairs = [[] for ip in range(I_PAIRS)]
        b_grouped_tiles = {}
        quantised_b = []

        def pair_of_a(ip, w):
            e = 2 * (w % 2)
            return a_grouped_pairs[ip][w // 2][:, e : e + 2, :, :]

        def turn_mask(ip, n):
            it = ip * PAIR + n
            mask_words = mik[:, it, :].bitcast(F32)
            maskT_ps = psum.tile([P, 2, P], F32, tag="bank")
            for u in range(2):
                nc.tensor.transpose(maskT_ps[:, u, :], mask_words[:, u : NK // 2 : 2], ident_f32[:])
            nc.scalar.copy(
                out=mikT[:, it, :, :].rearrange("p i t -> p (i t)").bitcast(F32).rearrange("p (i u) -> p i u", u=2),
                in_=maskT_ps[:].rearrange("p u i -> p i u"),
            )

        def turn_a(ip, n, ws=range(HALF)):
            it = ip * PAIR + n
            if not a_grouped_pairs[ip]:
                for h in range(2):
                    a_half = slabs.tile([P, HALF, PAIR * P, PACK], BF16, tag="slab", align_bytes=256)
                    a_grouped_pairs[ip].append(a_half)
            a_words = a_raw_tiles[it][:].bitcast(F32).rearrange("p (k w) -> p k w", w=HALF)
            pair_mask = mikT[:, it, :, :].unsqueeze(1).to_broadcast([P, 2, P, PACK])
            for w in ws:
                aT_ps = psum.tile([P, PACK * P], F32, tag="bank")
                for t in range(PACK):
                    nc.tensor.transpose(
                        aT_ps[:, t * P : (t + 1) * P], a_words[:, t:NK:PACK, w], ident_f32[:]
                    )
                pair = pair_of_a(ip, w)[:, :, n * P : (n + 1) * P, :]
                pair_T = aT_ps[:].bitcast(BF16).rearrange("p (t i e) -> p e i t", t=PACK, e=2)
                if w in A_ON_SCALAR[it]:
                    nc.scalar.copy(out=pair, in_=pair_T)
                else:
                    nc.vector.tensor_tensor(out=pair, in0=pair_T, in1=pair_mask, op=ALU.mult)

        def mask_a(ip, h):
            for w in range(2 * h, 2 * h + 2):
                tiles = [n for n in range(PAIR) if w in A_ON_SCALAR[ip * PAIR + n]]
                if not tiles:
                    continue
                i_cols = slice(tiles[0] * P, (tiles[-1] + 1) * P)
                pair = pair_of_a(ip, w)[:, :, i_cols, :].rearrange("p e i t -> p e (i t)")
                pair_mask = (
                    mikT[:, ip * PAIR + tiles[0] : ip * PAIR + tiles[-1] + 1, :, :]
                    .rearrange("p n i t -> p (n i t)")
                    .unsqueeze(1)
                    .to_broadcast([P, 2, len(tiles) * P * PACK])
                )
                nc.vector.tensor_tensor(out=pair, in0=pair, in1=pair_mask, op=ALU.mult)

        def quantise_a(ip, h):
            half = slice(h * HALF, (h + 1) * HALF)
            nc.vector.quantize_mx(
                out=a_codes[:, ip, half, :].rearrange("p d i -> p (d i)").bitcast(FP8X4),
                scales=a_scales[:, ip, half, :].rearrange("p d i -> p (d i)"),
                in_=a_grouped_pairs[ip][h][:].rearrange("p d i t -> p (d i t)"),
            )

        def regroup_b(jc, h, first=0, last=JC):
            if jc not in b_grouped_tiles:
                b_grouped = slabs.tile([P, ND, JC, PACK], BF16, tag="slab", align_bytes=256)
                b_grouped_tiles[jc] = b_grouped
            half = slice(h * HALF, (h + 1) * HALF)
            src = b_raw_tiles[jc][:].rearrange("p t j d -> p j t d")[:, first:last, :, half]
            dst = b_grouped_tiles[jc][:].rearrange("p d j t -> p j t d")[:, first:last, :, half]
            mask = mkj[:, :, jc * JC + first : jc * JC + last].rearrange("p t j -> p j t")
            mask = mask.unsqueeze(3).to_broadcast([P, last - first, PACK, HALF])
            if (jc, h) in B_ON_VECTOR:
                nc.vector.tensor_tensor(out=dst, in0=src, in1=mask, op=ALU.mult)
            else:
                nc.scalar.copy(out=dst, in_=src)

        def mask_b(jc, hs=(0, 1), first=0, last=JC):
            ds = slice(hs[0] * HALF, (hs[-1] + 1) * HALF)
            b_flat = b_grouped_tiles[jc][:, ds, first:last, :].rearrange("p d j t -> p d (j t)")
            mask = mkj_grouped[:, jc * JC + first : jc * JC + last, :].rearrange("p j t -> p (j t)")
            nc.vector.tensor_tensor(
                out=b_flat,
                in0=b_flat,
                in1=mask.unsqueeze(1).to_broadcast([P, len(hs) * HALF, (last - first) * PACK]),
                op=ALU.mult,
            )

        def quantise_b(jc):
            b_codes = b_mx.tile([P, ND, JC], U32, align_bytes=256)
            b_scales = b_mx.tile([P, ND, JC], U8, align_bytes=256)
            nc.vector.quantize_mx(
                out=b_codes[:].rearrange("p d j -> p (d j)").bitcast(FP8X4),
                scales=b_scales[:].rearrange("p d j -> p (d j)"),
                in_=b_grouped_tiles[jc][:].rearrange("p d j t -> p (d j t)"),
            )
            quantised_b.append((b_codes, b_scales))

        blocks = [(ip, jc) for jc in range(J_CHUNKS) for ip in range(I_PAIRS)]
        tiles_of = [dict() for block in blocks]

        def product(where, block, n, d, first, last):
            ip, jc = block
            b_codes, b_scales = quantised_b[jc]
            i_cols = slice(n * P, (n + 1) * P)
            nc.tensor.matmul_mx(
                out=where[:, n * JC : (n + 1) * JC],
                lhsT=a_codes[:, ip, d, i_cols].bitcast(FP8X4),
                lhsT_scale=a_scales[:, ip, d, i_cols],
                rhs=b_codes[:, d, :].bitcast(FP8X4),
                rhs_scale=b_scales[:, d, :],
                start=first,
                stop=last,
            )

        def product_T(where, block, d):
            ip, jc = block
            b_codes, b_scales = quantised_b[jc]
            nc.tensor.matmul_mx(
                out=where,
                lhsT=b_codes[:, d, :].bitcast(FP8X4),
                lhsT_scale=b_scales[:, d, :],
                rhs=a_codes[:, ip, d, :].bitcast(FP8X4),
                rhs_scale=a_scales[:, ip, d, :],
                start=True,
                stop=True,
            )

        def squares(m, q):
            if q == 0:
                squares_T = slabs.tile([P, ND, BLOCK], F32, tag="slab", align_bytes=256)
                tiles_of[m].update(squares_T=squares_T)
            x_ps = psum.tile([P, 2, BLOCK], F32, tag="bank")
            for e in range(2):
                product_T(x_ps[:, e, :], blocks[m], 2 * q + e)
            nc.scalar.activation(
                out=tiles_of[m]["squares_T"][:, 2 * q : 2 * q + 2, :], in_=x_ps[:], func=ACT.Square
            )

        def every_square(m):
            for q in range(HALF):
                squares(m, q)

        def sum_squares(m):
            squares_T = tiles_of[m]["squares_T"]
            sums_ps = tiles_of[m]["sums_ps"]
            for n in range(PAIR):
                cols = slice(n * JC, (n + 1) * JC)
                for d in range(ND):
                    nc.tensor.matmul(
                        out=sums_ps[:, 0, cols],
                        lhsT=squares_T[:, d, n * P : (n + 1) * P],
                        rhs=ident_f32[:],
                        is_transpose=True,
                        start=(d == 0),
                        stop=(d == ND - 1),
                    )

        def sum_products(m):
            sums_ps = stats.tile([P, 2, BLOCK], F32)
            tiles_of[m].update(sums_ps=sums_ps)
            for n in range(PAIR):
                for d in range(ND):
                    product(sums_ps[:, 1, :], blocks[m], n, d, d == 0, d == ND - 1)

        def sums(m):
            sum_products(m)
            sum_squares(m)

        def mean_squared(m):
            mean_sq = ln.tile([P, BLOCK], F32, align_bytes=256)
            nc.scalar.activation(
                out=mean_sq[:], in_=tiles_of[m]["sums_ps"][:, 1, :], func=ACT.Square, scale=1.0 / ND
            )
            tiles_of[m].update(mean_sq=mean_sq)

        def variance(m):
            var = ln.tile([P, BLOCK], F32, align_bytes=256)
            nc.vector.scalar_tensor_tensor(
                out=var[:],
                in0=tiles_of[m]["sums_ps"][:, 0, :],
                scalar=1.0 / ND,
                in1=tiles_of[m]["mean_sq"][:],
                op0=ALU.mult,
                op1=ALU.subtract,
            )
            tiles_of[m].update(var=var)

        def reciprocal_std(m):
            rstd = ln.tile([P, BLOCK], F32, align_bytes=256)
            nc.scalar.activation(
                out=rstd[:], in_=tiles_of[m]["var"][:], func=ACT.Abs_reciprocal_sqrt, bias=eps_col[:, 0:1]
            )
            tiles_of[m].update(rstd=rstd)

        def minus_mean_times_rstd(m):
            neg_mean_rstd = ln.tile([P, BLOCK], F32, align_bytes=256)
            nc.vector.scalar_tensor_tensor(
                out=neg_mean_rstd[:],
                in0=tiles_of[m]["sums_ps"][:, 1, :],
                scalar=-1.0 / ND,
                in1=tiles_of[m]["rstd"][:],
                op0=ALU.mult,
                op1=ALU.mult,
            )
            tiles_of[m].update(neg_mean_rstd=neg_mean_rstd)

        def shifts(m, part):
            if part == 0:
                shift = slabs.tile([P, BLOCK // RUN, ND, RUN], F32, tag="slab", align_bytes=256)
                tiles_of[m].update(shift=shift)
            count = SHIFTS_ON_SCALAR[m]
            for d in range(count // 2) if part == 0 else range(count // 2, count):
                nc.scalar.activation(
                    out=tiles_of[m]["shift"][:, :, d, :],
                    in_=tiles_of[m]["neg_mean_rstd"][:].rearrange("p (c i) -> p c i", i=RUN),
                    func=ACT.Identity,
                    scale=w_col[:, d : d + 1],
                    bias=bias_col[:, d : d + 1],
                )

        def shift_on_vector(m, d, cols):
            nc.vector.tensor_scalar(
                out=tiles_of[m]["shift"][:, cols.start // RUN : cols.stop // RUN, d, :],
                in0=tiles_of[m]["neg_mean_rstd"][:, cols].rearrange("p (c i) -> p c i", i=RUN),
                scalar1=w_col[:, d : d + 1],
                scalar2=bias_col[:, d : d + 1],
                op0=ALU.mult,
                op1=ALU.add,
            )

        def scale_products(m):
            scaled = slabs.tile([P, BLOCK // RUN, ND, RUN], F32, tag="slab", align_bytes=256)
            for q in range(HALF):
                x_ps = psum.tile([P, 2, BLOCK], F32, tag="bank")
                for e in range(2):
                    for n in range(PAIR):
                        product(x_ps[:, e, :], blocks[m], n, 2 * q + e, True, True)
                for e in range(2):
                    d = 2 * q + e
                    nc.vector.scalar_tensor_tensor(
                        out=scaled[:, :, d, :],
                        in0=x_ps[:, e, :].rearrange("p (c i) -> p c i", i=RUN),
                        scalar=w_col[:, d : d + 1],
                        in1=tiles_of[m]["rstd"][:].rearrange("p (c i) -> p c i", i=RUN),
                        op0=ALU.mult,
                        op1=ALU.mult,
                    )
            tiles_of[m].update(scaled=scaled)

        def shifts_on_vector(m):
            last = m == len(blocks) - 1
            for d in range(SHIFTS_ON_SCALAR[m], ND if last else ND - 1):
                shift_on_vector(m, d, slice(0, BLOCK))
            if not last:
                shift_on_vector(m, ND - 1, slice(GPSIMD_COLUMNS, BLOCK))

        def add_shifts_and_store(m):
            if m == len(blocks) - 1:
                width = JC // LAST_PARTS
                for first in range(0, BLOCK, width):
                    add(m, nc.vector, first, first + width)
                return
            add(m, nc.vector, GPSIMD_COLUMNS, BLOCK)
            shift_on_vector(m, ND - 1, slice(0, GPSIMD_COLUMNS))
            add(m, nc.gpsimd, 0, GPSIMD_COLUMNS)

        def add(m, engine, first, last):
            ip, jc = blocks[m]
            groups = slice(first // RUN, last // RUN)
            result = results.tile([P, last - first, ND], F32)
            engine.tensor_tensor(
                out=result[:].rearrange("p (c i) d -> p c d i", i=RUN),
                in0=tiles_of[m]["scaled"][:, groups, :, :],
                in1=tiles_of[m]["shift"][:, groups, :, :],
                op=ALU.add,
            )
            for n in range(first // JC, (last - 1) // JC + 1):
                start, end = max(first, n * JC), min(last, (n + 1) * JC)
                at = (jc * JC + start - n * JC) * ND
                nc.sync.dma_start(
                    out=out_rows[ip * PAIR + n, :, at : at + (end - start) * ND],
                    in_=result[:, start - first : end - first, :].rearrange("p j d -> p (j d)"),
                )

        def group_mask_kj(jc):
            cols = slice(jc * JC, (jc + 1) * JC)
            nc.gpsimd.tensor_scalar(
                out=mkj_grouped[:, cols, :],
                in0=mkj[:, :, cols].rearrange("p t j -> p j t"),
                scalar1=1.0,
                scalar2=0.0,
                op0=ALU.mult,
                op1=ALU.add,
            )

        def columns():
            nc.gpsimd.tensor_copy(out=w_col[:], in_=w_bf16[:])
            nc.gpsimd.tensor_copy(out=bias_col[:], in_=bias_bf16[:])

        group_mask_kj(0)
        group_mask_kj(1)
        regroup_b(0, 0, 0, JC // 2)
        regroup_b(0, 1, 0, JC // 2)
        mask_b(0, (1,), 0, JC // 2)
        turn_mask(0, 0)
        regroup_b(0, 0, JC // 2)
        turn_a(0, 0)
        group_mask_kj(3)
        turn_mask(0, 1)
        regroup_b(0, 1, JC // 2)
        mask_b(0, (1,), JC // 2, JC)
        turn_a(0, 1, (0, 1))
        quantise_b(0)
        turn_a(0, 1, (2, 3))
        mask_a(0, 0)
        mask_a(0, 1)
        quantise_a(0, 0)
        quantise_a(0, 1)
        turn_mask(1, 0)
        turn_a(1, 0)
        turn_mask(1, 1)
        turn_a(1, 1)
        every_square(0)
        columns()
        mask_a(1, 0)
        mask_a(1, 1)
        quantise_a(1, 0)
        quantise_a(1, 1)
        regroup_b(1, 0)
        regroup_b(1, 1)
        sum_products(0)
        sum_squares(0)
        mean_squared(0)
        every_square(1)
        mask_b(1)
        variance(0)
        quantise_b(1)
        reciprocal_std(0)
        regroup_b(3, 0)
        sum_products(1)
        sum_squares(1)
        mean_squared(1)
        every_square(2)
        regroup_b(2, 0)
        minus_mean_times_rstd(0)
        variance(1)
        reciprocal_std(1)
        shifts(0, 0)
        shifts(0, 1)
        sum_products(2)
        sum_squares(2)
        mean_squared(2)
        regroup_b(2, 1)
        every_square(3)
        minus_mean_times_rstd(1)
        quantise_b(2)
        regroup_b(3, 1)
        mask_b(3, (0,))
        variance(2)
        quantise_b(3)


        def stage(work, m, *which):
            if m < len(blocks):
                work(m, *which)

        for m in range(len(blocks)):
            stage(scale_products, m)
            stage(reciprocal_std, m + 2)
            stage(shifts, m + 1, 0)
            stage(shifts, m + 1, 1)
            stage(sum_products, m + 3)
            stage(sum_squares, m + 3)
            stage(mean_squared, m + 3)
            stage(every_square, m + 4)
            if m == 0:
                shifts_on_vector(m)
            stage(minus_mean_times_rstd, m + 2)
            stage(shifts_on_vector, m + 1)
            add_shifts_and_store(m)
            stage(variance, m + 3)
